import numpy as np
import ml_dtypes


def mxq(x, axis, fmt="e4m3"):
    dtype, down = {"e4m3": (ml_dtypes.float8_e4m3fn, 7), "e5m2": (ml_dtypes.float8_e5m2, 14)}[fmt]
    v = np.moveaxis(np.asarray(x, np.float32).astype(ml_dtypes.bfloat16).astype(np.float64), axis, -1)
    blocks = v.reshape(v.shape[:-1] + (-1, 32))
    amax = np.abs(blocks).max(-1, keepdims=True)
    byte = np.maximum(np.where(amax > 0, np.frexp(amax)[1] - 1 + 127, 0) - down, 1)
    scale = np.exp2(byte - 127.0)
    codes = (blocks / scale).astype(np.float32).astype(dtype).astype(np.float64)
    return np.moveaxis((codes * scale).reshape(v.shape), -1, axis)


WIDE = False


def mx_kscale(k):
    if not WIDE:
        return np.ones(k)
    levels = np.array([10, -10, 5, -5, 0])
    a = np.random.permutation(np.resize(levels, k // 512 * 4)).reshape(k // 512, 4)
    idx = np.arange(k)
    return np.exp2(a[idx // 512, idx % 128 // 32])


BF16 = ml_dtypes.bfloat16


def bf(x):
    return np.asarray(x, np.float32).astype(BF16)


def f64(x):
    return np.asarray(x).astype(np.float64)


N0, N1, N2, N3, D = 4096, 1024, 64, 16, 512
SIGMA = 2.0


def setup_inputs():
    s = mx_kscale(D)
    s = s / s.min()
    return {"task_embedding": bf(np.random.standard_normal((N0, D)) * 0.5 * s),
            "centers1": bf(np.random.random_sample((N1, D)) * 8.0 / np.sqrt(D) / s),
            "W1": bf(np.random.standard_normal((D, D)) * 2.0 / np.sqrt(D) / s),
            "b1": bf(np.random.standard_normal(D) * 0.1)}


def reference(task_embedding, centers1, W1, b1):
    c = f64(centers1)
    hq = mxq(f64(task_embedding), 1, "e4m3")
    g = hq @ mxq(c, 1, "e4m3").T
    sq = -2.0 * g + (c * c).sum(1)[None, :]
    l = -sq / (2.0 * SIGMA)
    e = np.exp(l - l.max(1, keepdims=True))
    p = e / e.sum(1, keepdims=True)
    t = np.tanh((hq @ mxq(f64(W1), 1, "e4m3").T) + f64(b1))
    return mxq(p, 0, "e4m3").T @ mxq(t, 0, "e4m3")

@@ -1,0 +1,492 @@
+from contextlib import ExitStack
+
+import concourse.mybir as mybir
+from concourse.masks import make_identity
+
+FLOPS = 2 * 4096 * 512 * 1024 + 2 * 4096 * 512 * 512 + 2 * 4096 * 1024 * 512
+
+F32 = mybir.dt.float32
+BF16 = mybir.dt.bfloat16
+U32 = mybir.dt.uint32
+U8 = mybir.dt.uint8
+FP8X4 = mybir.dt.float8_e4m3fn_x4
+ACT = mybir.ActivationFunctionType
+ALU = mybir.AluOpType
+AX = mybir.AxisListType
+
+P = 128
+NG = 8
+NA = 8
+NS = 32
+NARROW = 28
+POOL_PER_SLOT = 6
+DV = 1
+
+
+def tile_hierarchicalclustering_pa_t_kernel(tc, task_embedding, centers1, W1, b1, out):
+    nc = tc.nc
+    h_view = task_embedding.rearrange("(g p t) k -> g p (t k)", p=P, t=4)
+    c_view = centers1.rearrange("(p a) k -> p a k", a=NA)
+    w_view = W1.rearrange("(a p) k -> p a k", p=P)
+    out_view = out.rearrange("(p a) d -> p a d", a=NA)
+
+    with ExitStack() as ctx:
+        ctx.enter_context(tc.manual_schedule())
+        keep = ctx.enter_context(tc.tile_pool(name="keep", bufs=1))
+        hpool = ctx.enter_context(tc.tile_pool(name="hpool", bufs=4))
+        spool = ctx.enter_context(tc.tile_pool(name="spool", bufs=3))
+        gh = ctx.enter_context(tc.tile_pool(name="gh", bufs=2))
+        small = ctx.enter_context(tc.tile_pool(name="small", bufs=4))
+        psum = ctx.enter_context(tc.psum_pool(name="psum", bufs=1))
+
+        def bank(i, shape, dtype, name):
+            return psum.tile(shape, dtype, tag="b%d" % i, name=name)
+
+        ident_f = keep.tile([P, P], F32)
+        ident_b = keep.tile([P, P], BF16)
+        hc = keep.tile([P, NG, 512], U32, align_bytes=64)
+        hs = keep.tile([P, NG, 512], U8, align_bytes=64)
+        cc = keep.tile([P, 1024], U32, align_bytes=64)
+        cs = keep.tile([P, 1024], U8, align_bytes=64)
+        wc = keep.tile([P, 512], U32, align_bytes=64)
+        ws = keep.tile([P, 512], U8, align_bytes=64)
+        pc = keep.tile([P, NG, 1024], U32, align_bytes=64)
+        ps = keep.tile([P, NG, 1024], U8, align_bytes=64)
+        tcod = keep.tile([P, NG, 512], U32, align_bytes=64)
+        tsc = keep.tile([P, NG, 512], U8, align_bytes=64)
+        c4b = keep.tile([P, 1024], F32)
+        b1c = keep.tile([P, 4], F32)
+
+        hraw = {}
+        hgrps = {}
+        xbanks = {}
+        gps = {}
+        tTs = {}
+        tgrps = {}
+        ses = {}
+        mns = {}
+        sms = {}
+        rinvs = {}
+        pgrps = {}
+
+        def load_h(g):
+            hraw[g] = hpool.tile([P, 2048], BF16, tag="hraw", name="hraw%d" % g)
+            nc.sync.dma_start(out=hraw[g][:], in_=h_view[g])
+
+        def pe_t(g, half, b):
+            hw = hraw[g][:].bitcast(F32)
+            xh = bank(b, [P, 2, 2, P], F32, "xh%d_%d" % (g, half))
+            for tl in range(2):
+                for u in range(2):
+                    lo = (2 * half + tl) * 256 + u * 128
+                    nc.tensor.transpose(xh[:, tl, u, :], hw[:, lo : lo + 128], ident_f[:])
+            xbanks[("t", g, half)] = xh
+
+        def s_t(g, half):
+            if half == 0:
+                hgrps[g] = gh.tile([P, 2048], BF16, tag="hgrp", name="hgrp%d" % g, align_bytes=64)
+            hgw = hgrps[g][:].bitcast(F32).rearrange("q (t j u) -> q t j u", t=4, u=2)
+            nc.scalar.copy(
+                out=hgw[:, 2 * half : 2 * half + 2, :, :],
+                in_=xbanks[("t", g, half)][:].rearrange("q t u j -> q t j u"),
+            )
+
+        def v_qh(g):
+            nc.vector.quantize_mx(out=hc[:, g, :].bitcast(FP8X4), scales=hs[:, g, :], in_=hgrps[g][:])
+
+        def pe_z(g, dt, b):
+            z = bank(b, [P, 512], F32, "z%d_%d" % (g, dt))
+            nc.tensor.matmul_mx(
+                out=z[:],
+                lhsT=wc[:, dt * P : (dt + 1) * P].bitcast(FP8X4),
+                lhsT_scale=ws[:, dt * P : (dt + 1) * P],
+                rhs=hc[:, g, :].bitcast(FP8X4),
+                rhs_scale=hs[:, g, :],
+                start=True,
+                stop=True,
+            )
+            xbanks[("z", g, dt)] = z
+
+        def s_z(g, dt):
+            if dt == 0:
+                tTs[g] = grp.tile([P, 4, 512], BF16, tag="tT", name="tT%d" % g)
+            nc.scalar.activation(
+                out=tTs[g][:, dt, :], in_=xbanks[("z", g, dt)][:], func=ACT.Tanh,
+                bias=b1c[:, dt : dt + 1], scale=1.0,
+            )
+
+        def pe_x(g, hb, b):
+            xt = bank(b, [P, 4, 256], BF16, "xt%d_%d" % (g, hb))
+            for dl in range(2):
+                for t in range(4):
+                    nc.tensor.transpose(
+                        xt[:, t, dl * P : (dl + 1) * P], tTs[g][:, 2 * hb + dl, t * P : (t + 1) * P], ident_b[:]
+                    )
+            xbanks[("x", g, hb)] = xt
+
+        def s_x(g, hb):
+            if hb == 0:
+                tgrps[g] = grp.tile([P, 512, 4], BF16, tag="tgrp", name="tgrp%d" % g, align_bytes=64)
+            nc.scalar.copy(
+                out=tgrps[g][:, hb * 256 : (hb + 1) * 256, :],
+                in_=xbanks[("x", g, hb)][:].rearrange("p t d -> p d t"),
+            )
+
+        def v_qt(g):
+            nc.vector.quantize_mx(
+                out=tcod[:, g, :].bitcast(FP8X4), scales=tsc[:, g, :],
+                in_=tgrps[g][:].rearrange("p d t -> p (d t)"),
+            )
+
+        def g_banks(s):
+            if s >= NARROW:
+                return (0, 1)
+            return ((2 * s) % 4, (2 * s) % 4 + 1)
+
+        def pe_g(s):
+            g, t = divmod(s, 4)
+            for hf in range(2):
+                gp = bank(g_banks(s)[hf], [P, 512], F32, "gp%d_%d" % (s, hf))
+                nc.tensor.matmul_mx(
+                    out=gp[:],
+                    lhsT=hc[:, g, t * P : (t + 1) * P].bitcast(FP8X4),
+                    lhsT_scale=hs[:, g, t * P : (t + 1) * P],
+                    rhs=cc[:, hf * 512 : (hf + 1) * 512].bitcast(FP8X4),
+                    rhs_scale=cs[:, hf * 512 : (hf + 1) * 512],
+                    start=True,
+                    stop=True,
+                )
+                gps[(s, hf)] = gp
+
+        def v_ab(s):
+            g, t = divmod(s, 4)
+            if t == 0:
+                ses[g] = spool.tile([P, 4, 1024], F32, tag="se", name="se%d" % g)
+                mns[g] = small.tile([P, 4], F32, tag="mn", name="mn%d" % g)
+            for hf in range(2):
+                nc.vector.scalar_tensor_tensor(
+                    out=ses[g][:, t, hf * 512 : (hf + 1) * 512], in0=gps[(s, hf)][:], scalar=-0.5,
+                    in1=c4b[:, hf * 512 : (hf + 1) * 512], op0=ALU.mult, op1=ALU.add,
+                )
+            nc.vector.tensor_reduce(out=mns[g][:, t : t + 1], in_=ses[g][:, t, :], axis=AX.X, op=ALU.min)
+
+        def s_c(s):
+            g, t = divmod(s, 4)
+            if t == 0:
+                sms[g] = small.tile([P, 4], F32, tag="sm", name="sm%d" % g)
+            nc.scalar.activation(
+                out=ses[g][:, t, :], in_=ses[g][:, t, :], func=ACT.Exp, bias=mns[g][:, t : t + 1], scale=-1.0,
+                accum_out=sms[g][:, t : t + 1],
+            )
+
+        def v_r(g):
+            rinvs[g] = small.tile([P, 4], F32, tag="rinv", name="rinv%d" % g)
+            nc.vector.reciprocal(rinvs[g][:], sms[g][:])
+            pgrps[g] = grp.tile([P, 1024, 4], BF16, tag="pgrp", name="pgrp%d" % g, align_bytes=64)
+
+        def d_piece(eng, g, lo, n):
+            eng.tensor_tensor(
+                out=pgrps[g][:, lo : lo + n, :],
+                in0=ses[g][:, :, lo : lo + n].rearrange("p t i -> p i t"),
+                in1=rinvs[g][:].unsqueeze(1).to_broadcast([P, n, 4]),
+                op=ALU.mult,
+            )
+
+        def d_scalar(g, lo, n):
+            for t in range(4):
+                nc.scalar.activation(
+                    out=pgrps[g][:, lo : lo + n, t], in_=ses[g][:, t, lo : lo + n], func=ACT.Copy,
+                    scale=rinvs[g][:, t : t + 1],
+                )
+
+        def v_qp(g, lo, n):
+            nc.vector.quantize_mx(
+                out=pc[:, g, lo : lo + n].bitcast(FP8X4), scales=ps[:, g, lo : lo + n],
+                in_=pgrps[g][:, lo : lo + n, :].rearrange("p i t -> p (i t)"),
+            )
+
+        accs = {}
+        done = {}
+
+        def pool_pass(a, g):
+            nc.tensor.matmul_mx(
+                out=accs[a][:],
+                lhsT=pc[:, g, a * P : (a + 1) * P].bitcast(FP8X4),
+                lhsT_scale=ps[:, g, a * P : (a + 1) * P],
+                rhs=tcod[:, g, :].bitcast(FP8X4),
+                rhs_scale=tsc[:, g, :],
+                start=(g == 0),
+                stop=(g == NG - 1),
+            )
+            done[a] = g + 1
+
+        def open_acc(a, b):
+            accs[a] = bank(b, [P, 512], F32, "acc%d" % a)
+            done[a] = 0
+
+        ready = {"p": [0] * NA, "t": 0}
+
+        def pool_some(limit):
+            n = 0
+            for a in sorted(accs):
+                while n < limit and done[a] < min(ready["p"][a], ready["t"]):
+                    pool_pass(a, done[a])
+                    n += 1
+
+        def mark_p(g, a_lo, a_hi):
+            for a in range(a_lo, a_hi):
+                ready["p"][a] = g + 1
+
+        make_identity(nc, ident_f[:])
+        with tc.tile_pool(name="head", bufs=1) as head:
+            b1rows = head.tile([P, P], BF16)
+            nc.gpsimd.memset(b1rows[:], 0.0)
+            make_identity(nc, ident_b[:])
+            c_sb = head.tile([P, NA, 512], BF16)
+            for k in range(4):
+                nc.sync.dma_start(out=c_sb[:, 2 * k : 2 * k + 2, :], in_=c_view[:, 2 * k : 2 * k + 2, :])
+            load_h(0)
+            w_sb = head.tile([P, 4, 512], BF16)
+            nc.sync.dma_start(out=w_sb[:], in_=w_view)
+            nc.sync.dma_start(out=b1rows[0:4, :], in_=b1.rearrange("(a p) -> a p", p=P))
+            load_h(1)
+            load_h(2)
+            load_h(3)
+
+            cw = c_sb[:].rearrange("p a k -> p (a k)").bitcast(F32)
+            cgrp = head.tile([P, 4096], BF16, align_bytes=64)
+            cgw = cgrp[:].bitcast(F32).rearrange("q (a j u) -> q a j u", a=NA, u=2)
+            csq_s = head.tile([P, 4], F32)
+            csq_v = head.tile([P, 4], F32)
+            junk_s = head.tile([P, 512], F32)
+            junk_v = head.tile([P, 512], F32)
+            rep = head.tile([P, 4, 2, P], F32)
+            xcs = []
+            xrs = []
+
+            def pe_c(k):
+                xc = bank(k, [P, 2, 2, P], F32, "xc%d" % k)
+                for al in range(2):
+                    for u in range(2):
+                        lo = (2 * k + al) * 256 + u * 128
+                        nc.tensor.transpose(xc[:, al, u, :], cw[:, lo : lo + 128], ident_f[:])
+                xcs.append(xc)
+
+            def csq(k):
+                nc.scalar.activation(
+                    out=junk_s[:], in_=c_sb[:, 2 * k, :], func=ACT.Square, accum_out=csq_s[:, k : k + 1]
+                )
+                nc.vector.scalar_tensor_tensor(
+                    out=junk_v[:], in0=c_sb[:, 2 * k + 1, :], scalar=1.0, in1=c_sb[:, 2 * k + 1, :],
+                    op0=ALU.mult, op1=ALU.mult, accum_out=csq_v[:, k : k + 1],
+                )
+
+            def v_rep(hf):
+                for par, src in ((0, csq_s), (1, csq_v)):
+                    nc.gpsimd.tensor_scalar(
+                        out=rep[:, 2 * hf : 2 * hf + 2, par, :],
+                        in0=src[:, 2 * hf : 2 * hf + 2].unsqueeze(2).to_broadcast([P, 2, P]),
+                        scalar1=0.25, scalar2=0.0, op0=ALU.mult, op1=ALU.add,
+                    )
+
+            def pe_rep(hf):
+                xr = bank(6 + hf, [P, 4, P], F32, "xr%d" % hf)
+                for al in range(4):
+                    nc.tensor.transpose(xr[:, al, :], rep[:, 2 * hf + al // 2, al % 2, :], ident_f[:])
+                xrs.append(xr)
+
+            def c_evac(eng_copy, k):
+                eng_copy(out=cgw[:, 2 * k : 2 * k + 2, :, :], in_=xcs[k][:].rearrange("q a u j -> q a j u"))
+
+            def c4b_evac(eng_copy, hf):
+                eng_copy(out=c4b[:, hf * 512 : (hf + 1) * 512], in_=xrs[hf][:].rearrange("p a j -> p (a j)"))
+
+            def v_qc(hf):
+                nc.vector.quantize_mx(
+                    out=cc[:, hf * 512 : (hf + 1) * 512].bitcast(FP8X4), scales=cs[:, hf * 512 : (hf + 1) * 512],
+                    in_=cgrp[:, hf * 2048 : (hf + 1) * 2048],
+                )
+
+            pe_c(0)
+            csq(0)
+            pe_c(1)
+            csq(1)
+            v_rep(0)
+            pe_c(2)
+            csq(2)
+            pe_rep(0)
+            pe_c(3)
+            csq(3)
+            v_rep(1)
+            pe_t(0, 0, 4)
+            pe_t(0, 1, 5)
+            pe_rep(1)
+            c_evac(nc.scalar.copy, 0)
+            c_evac(nc.scalar.copy, 1)
+            c_evac(nc.vector.tensor_copy, 2)
+            c_evac(nc.vector.tensor_copy, 3)
+            v_qc(0)
+            c4b_evac(nc.vector.tensor_copy, 0)
+            s_t(0, 0)
+            s_t(0, 1)
+            v_qh(0)
+            c4b_evac(nc.scalar.copy, 1)
+            v_qc(1)
+
+            ww = w_sb[:].rearrange("p a k -> p (a k)").bitcast(F32)
+            wgrp = head.tile([P, 2048], BF16, align_bytes=64)
+            wgw = wgrp[:].bitcast(F32).rearrange("q (a j u) -> q a j u", a=4, u=2)
+            xws = []
+            for pair in range(2):
+                xw = bank(4 + pair, [P, 2, 2, P], F32, "xw%d" % pair)
+                for al in range(2):
+                    for u in range(2):
+                        lo = (2 * pair + al) * 256 + u * 128
+                        nc.tensor.transpose(xw[:, al, u, :], ww[:, lo : lo + 128], ident_f[:])
+                xws.append(xw)
+            pe_g(0)
+            pe_g(1)
+            for pair in range(2):
+                nc.scalar.copy(
+                    out=wgw[:, 2 * pair : 2 * pair + 2, :, :], in_=xws[pair][:].rearrange("q a u j -> q a j u")
+                )
+            xb = bank(4, [P, P], BF16, "xb")
+            nc.tensor.transpose(xb[:], b1rows[:], ident_b[:])
+            nc.scalar.copy(out=b1c[:], in_=xb[:, 0:4])
+
+            def v_qw():
+                nc.vector.quantize_mx(out=wc[:].bitcast(FP8X4), scales=ws[:], in_=wgrp[:])
+
+            v_ab(0)
+            v_qw()
+
+        grp = ctx.enter_context(tc.tile_pool(name="grp", bufs=2))
+        ostage = ctx.enter_context(tc.tile_pool(name="ostage", bufs=8))
+
+        units = []
+
+        def add_t(g):
+            units.append((lambda b: pe_t(g, 0, b), lambda: s_t(g, 0), None))
+            units.append((lambda b: pe_t(g, 1, b), lambda: s_t(g, 1), lambda: v_qh(g)))
+
+        def add_z(g, d0):
+            units.append((lambda b: pe_z(g, d0, b), lambda: s_z(g, d0), None))
+            units.append((lambda b: pe_z(g, d0 + 1, b), lambda: s_z(g, d0 + 1), None))
+
+        def qt_and_mark(g):
+            v_qt(g)
+            ready["t"] = g + 1
+
+        def add_x(g):
+            units.append((lambda b: pe_x(g, 0, b), lambda: s_x(g, 0), None))
+            units.append((lambda b: pe_x(g, 1, b), lambda: s_x(g, 1), lambda: qt_and_mark(g)))
+
+        add_t(1)
+        add_z(0, 0)
+        add_z(0, 2)
+        for gam in range(1, NG):
+            if gam + 1 < NG:
+                add_t(gam + 1)
+            add_x(gam - 1)
+            add_z(gam, 0)
+            add_z(gam, 2)
+        add_x(NG - 1)
+
+        state = {"pe": 0, "s": 0, "v": 0}
+        vq = []
+
+        def pe_pair(n=2):
+            for i in range(n):
+                if state["pe"] < len(units):
+                    units[state["pe"]][0](5 - (state["pe"] % 2))
+                    state["pe"] += 1
+
+        def s_pair(n=2):
+            for i in range(n):
+                if state["s"] < state["pe"]:
+                    units[state["s"]][1]()
+                    if units[state["s"]][2] is not None:
+                        vq.append(units[state["s"]][2])
+                    state["s"] += 1
+
+        def v_pending():
+            while state["v"] < len(vq):
+                vq[state["v"]]()
+                state["v"] += 1
+
+        G_N = 1024 - DV * P
+
+        def window(g):
+            if g >= 2:
+                if DV > 0:
+                    d_piece(nc.vector, g - 2, G_N, DV * P)
+                v_qp(g - 2, 0, 1024)
+                mark_p(g - 2, 0, NA)
+            v_pending()
+            v_r(g - 1)
+
+        open_acc(0, 6)
+        open_acc(1, 7)
+
+        pe_pair()
+        for s in range(NS):
+            g, t = divmod(s, 4)
+            if s > 0:
+                v_ab(s)
+                s_c(s - 1)
+            if g == 0:
+                v_pending()
+            elif t == 0:
+                window(g)
+                d_piece(nc.gpsimd, g - 1, 0, G_N // 2)
+                d_piece(nc.gpsimd, g - 1, G_N // 2, G_N // 2)
+            if s + 2 <= NARROW:
+                pe_g(s + 2)
+            elif s == NARROW - 1:
+                open_acc(4, 2)
+                open_acc(5, 3)
+            elif s + 1 < NS:
+                pe_g(s + 1)
+            else:
+                open_acc(6, 0)
+                open_acc(7, 1)
+            s_pair(3)
+            pe_pair(3 if t == 0 and g >= 1 else 2)
+            if state["s"] == len(units) and 2 not in accs:
+                open_acc(2, 4)
+                open_acc(3, 5)
+            if s == 0:
+                load_h(4)
+                load_h(5)
+            if s == 3:
+                load_h(6)
+            if s == 7:
+                load_h(7)
+            pool_some(POOL_PER_SLOT)
+
+        s_c(NS - 1)
+        s_pair(100)
+        if 2 not in accs:
+            open_acc(2, 4)
+            open_acc(3, 5)
+        pool_some(100)
+        window(NG)
+        pool_some(100)
+
+        def finish(a):
+            ot = ostage.tile([P, 512], F32, tag="ot", name="ot%d" % a)
+            if a < NA - 1:
+                nc.scalar.copy(out=ot[:], in_=accs[a][:])
+            else:
+                nc.vector.tensor_copy(out=ot[:], in_=accs[a][:])
+            nc.sync.dma_start(out=out_view[:, a, :], in_=ot[:])
+
+        d_scalar(NG - 1, 768, 256)
+        for q in range(4):
+            if q < 3:
+                d_piece(nc.vector, NG - 1, q * 256, 256)
+            v_qp(NG - 1, q * 256, 256)
+            mark_p(NG - 1, 2 * q, 2 * q + 2)
+            pool_some(100)
+            finish(2 * q)
+            finish(2 * q + 1)

@@ -20,7 +20,8 @@ NA = 8
 NS = 32
 NARROW = 28
 POOL_PER_SLOT = 6
-DV = 1
+DV = 0
+DS = 0
 
 
 def tile_hierarchicalclustering_pa_t_kernel(tc, task_embedding, centers1, W1, b1, out):
@@ -414,12 +415,12 @@ def tile_hierarchicalclustering_pa_t_kernel(tc, task_embedding, centers1, W1, b1
                 vq[state["v"]]()
                 state["v"] += 1
 
-        G_N = 1024 - DV * P
+        G_N = 1024 - (DV + DS) * P
 
         def window(g):
             if g >= 2:
                 if DV > 0:
-                    d_piece(nc.vector, g - 2, G_N, DV * P)
+                    d_piece(nc.vector, g - 2, 1024 - DV * P, DV * P)
                 v_qp(g - 2, 0, 1024)
                 mark_p(g - 2, 0, NA)
             v_pending()
@@ -440,6 +441,8 @@ def tile_hierarchicalclustering_pa_t_kernel(tc, task_embedding, centers1, W1, b1
                 window(g)
                 d_piece(nc.gpsimd, g - 1, 0, G_N // 2)
                 d_piece(nc.gpsimd, g - 1, G_N // 2, G_N // 2)
+                if DS > 0:
+                    d_scalar(g - 1, G_N, DS * P)
             if s + 2 <= NARROW:
                 pe_g(s + 2)
             elif s == NARROW - 1:

@@ -22,6 +22,8 @@ NARROW = 28
 POOL_PER_SLOT = 6
 DV = 0
 DS = 0
+DV_LATE = 1
+DS_LATE = 1
 
 
 def tile_hierarchicalclustering_pa_t_kernel(tc, task_embedding, centers1, W1, b1, out):
@@ -69,6 +71,7 @@ def tile_hierarchicalclustering_pa_t_kernel(tc, task_embedding, centers1, W1, b1
         sms = {}
         rinvs = {}
         pgrps = {}
+        pns = {}
 
         def load_h(g):
             hraw[g] = hpool.tile([P, 2048], BF16, tag="hraw", name="hraw%d" % g)
@@ -169,7 +172,10 @@ def tile_hierarchicalclustering_pa_t_kernel(tc, task_embedding, centers1, W1, b1
                     out=ses[g][:, t, hf * 512 : (hf + 1) * 512], in0=gps[(s, hf)][:], scalar=-0.5,
                     in1=c4b[:, hf * 512 : (hf + 1) * 512], op0=ALU.mult, op1=ALU.add,
                 )
-            nc.vector.tensor_reduce(out=mns[g][:, t : t + 1], in_=ses[g][:, t, :], axis=AX.X, op=ALU.min)
+            if s >= NARROW:
+                nc.vector.tensor_reduce(out=mns[g][:, t : t + 1], in_=ses[g][:, t, :], axis=AX.X, op=ALU.min)
+            elif t % 2 == 1:
+                nc.vector.tensor_reduce(out=mns[g][:, t - 1 : t + 1], in_=ses[g][:, t - 1 : t + 1, :], axis=AX.X, op=ALU.min)
 
         def s_c(s):
             g, t = divmod(s, 4)
@@ -193,12 +199,40 @@ def tile_hierarchicalclustering_pa_t_kernel(tc, task_embedding, centers1, W1, b1
                 op=ALU.mult,
             )
 
+        def d_scalar_t(g, lo, n, t):
+            nc.scalar.activation(
+                out=pgrps[g][:, lo : lo + n, t], in_=ses[g][:, t, lo : lo + n], func=ACT.Copy,
+                scale=rinvs[g][:, t : t + 1],
+            )
+
         def d_scalar(g, lo, n):
             for t in range(4):
-                nc.scalar.activation(
-                    out=pgrps[g][:, lo : lo + n, t], in_=ses[g][:, t, lo : lo + n], func=ACT.Copy,
-                    scale=rinvs[g][:, t : t + 1],
-                )
+                d_scalar_t(g, lo, n, t)
+
+        def v_r_tile(g, t):
+            if t == 0:
+                rinvs[g] = small.tile([P, 4], F32, tag="rinv", name="rinv%d" % g)
+                pns[g] = grp.tile([P, 4, 1024], BF16, tag="pn", name="pn%d" % g, bufs=1)
+                pgrps[g] = grp.tile([P, 1024, 4], BF16, tag="pgrp", name="pgrp%d" % g, align_bytes=64)
+            nc.vector.reciprocal(rinvs[g][:, t : t + 1], sms[g][:, t : t + 1])
+
+        def s_norm(g, t, lo, n):
+            nc.scalar.activation(
+                out=pns[g][:, t, lo : lo + n], in_=ses[g][:, t, lo : lo + n], func=ACT.Copy,
+                scale=rinvs[g][:, t : t + 1],
+            )
+
+        def v_norm(g, t, lo, n):
+            nc.vector.tensor_scalar(
+                out=pns[g][:, t, lo : lo + n], in0=ses[g][:, t, lo : lo + n], scalar1=rinvs[g][:, t : t + 1],
+                scalar2=None, op0=ALU.mult,
+            )
+
+        def v_regroup(g, lo, n):
+            nc.vector.tensor_copy(
+                out=pgrps[g][:, lo : lo + n, :].rearrange("p (c i) t -> p c t i", i=4),
+                in_=pns[g][:, :, lo : lo + n].rearrange("p t (c i) -> p c t i", i=4),
+            )
 
         def v_qp(g, lo, n):
             nc.vector.quantize_mx(
@@ -366,28 +400,35 @@ def tile_hierarchicalclustering_pa_t_kernel(tc, task_embedding, centers1, W1, b1
 
         units = []
 
+        h_ready = {0}
+
+        def qh_and_mark(g):
+            v_qh(g)
+            h_ready.add(g)
+
         def add_t(g):
-            units.append((lambda b: pe_t(g, 0, b), lambda: s_t(g, 0), None))
-            units.append((lambda b: pe_t(g, 1, b), lambda: s_t(g, 1), lambda: v_qh(g)))
+            units.append((lambda b: pe_t(g, 0, b), lambda: s_t(g, 0), None, None))
+            units.append((lambda b: pe_t(g, 1, b), lambda: s_t(g, 1), lambda: qh_and_mark(g), None))
 
         def add_z(g, d0):
-            units.append((lambda b: pe_z(g, d0, b), lambda: s_z(g, d0), None))
-            units.append((lambda b: pe_z(g, d0 + 1, b), lambda: s_z(g, d0 + 1), None))
+            units.append((lambda b: pe_z(g, d0, b), lambda: s_z(g, d0), None, g))
+            units.append((lambda b: pe_z(g, d0 + 1, b), lambda: s_z(g, d0 + 1), None, g))
 
         def qt_and_mark(g):
             v_qt(g)
             ready["t"] = g + 1
 
         def add_x(g):
-            units.append((lambda b: pe_x(g, 0, b), lambda: s_x(g, 0), None))
-            units.append((lambda b: pe_x(g, 1, b), lambda: s_x(g, 1), lambda: qt_and_mark(g)))
+            units.append((lambda b: pe_x(g, 0, b), lambda: s_x(g, 0), None, None))
+            units.append((lambda b: pe_x(g, 1, b), lambda: s_x(g, 1), lambda: qt_and_mark(g), None))
 
         add_t(1)
         add_z(0, 0)
         add_z(0, 2)
+        add_t(2)
         for gam in range(1, NG):
-            if gam + 1 < NG:
-                add_t(gam + 1)
+            if gam + 2 < NG:
+                add_t(gam + 2)
             add_x(gam - 1)
             add_z(gam, 0)
             add_z(gam, 2)
@@ -398,7 +439,7 @@ def tile_hierarchicalclustering_pa_t_kernel(tc, task_embedding, centers1, W1, b1
 
         def pe_pair(n=2):
             for i in range(n):
-                if state["pe"] < len(units):
+                if state["pe"] < len(units) and (units[state["pe"]][3] is None or units[state["pe"]][3] in h_ready):
                     units[state["pe"]][0](5 - (state["pe"] % 2))
                     state["pe"] += 1
 
@@ -415,16 +456,24 @@ def tile_hierarchicalclustering_pa_t_kernel(tc, task_embedding, centers1, W1, b1
                 vq[state["v"]]()
                 state["v"] += 1
 
-        G_N = 1024 - (DV + DS) * P
+        def ds_of(g):
+            return DS_LATE if g == NG - 2 else DS
+
+        def dv_of(g):
+            return DV_LATE if g == NG - 3 else DV
+
+        def g_n(g):
+            return 1024 - (dv_of(g) + ds_of(g)) * P
 
         def window(g):
             if g >= 2:
-                if DV > 0:
-                    d_piece(nc.vector, g - 2, 1024 - DV * P, DV * P)
+                if dv_of(g - 2) > 0:
+                    d_piece(nc.vector, g - 2, 1024 - dv_of(g - 2) * P, dv_of(g - 2) * P)
                 v_qp(g - 2, 0, 1024)
                 mark_p(g - 2, 0, NA)
             v_pending()
-            v_r(g - 1)
+            if g < NG:
+                v_r(g - 1)
 
         open_acc(0, 6)
         open_acc(1, 7)
@@ -434,15 +483,19 @@ def tile_hierarchicalclustering_pa_t_kernel(tc, task_embedding, centers1, W1, b1
             g, t = divmod(s, 4)
             if s > 0:
                 v_ab(s)
+            if s > NARROW:
+                s_c(s - 1)
+            elif t % 2 == 0 and s > 0:
+                s_c(s - 2)
                 s_c(s - 1)
             if g == 0:
                 v_pending()
-            elif t == 0:
+            elif (t == 1 and g < NG - 1) or (t == 0 and g == NG - 1):
                 window(g)
-                d_piece(nc.gpsimd, g - 1, 0, G_N // 2)
-                d_piece(nc.gpsimd, g - 1, G_N // 2, G_N // 2)
-                if DS > 0:
-                    d_scalar(g - 1, G_N, DS * P)
+                d_piece(nc.gpsimd, g - 1, 0, g_n(g - 1) // 2)
+                d_piece(nc.gpsimd, g - 1, g_n(g - 1) // 2, g_n(g - 1) // 2)
+                if ds_of(g - 1) > 0:
+                    d_scalar(g - 1, g_n(g - 1), ds_of(g - 1) * P)
             if s + 2 <= NARROW:
                 pe_g(s + 2)
             elif s == NARROW - 1:
@@ -453,8 +506,11 @@ def tile_hierarchicalclustering_pa_t_kernel(tc, task_embedding, centers1, W1, b1
             else:
                 open_acc(6, 0)
                 open_acc(7, 1)
+            if s > NARROW + 1:
+                v_r_tile(NG - 1, t - 2)
+                s_norm(NG - 1, t - 2, 0, 1024)
             s_pair(3)
-            pe_pair(3 if t == 0 and g >= 1 else 2)
+            pe_pair(3 if t == 1 and g >= 1 else 2)
             if state["s"] == len(units) and 2 not in accs:
                 open_acc(2, 4)
                 open_acc(3, 5)
@@ -463,7 +519,7 @@ def tile_hierarchicalclustering_pa_t_kernel(tc, task_embedding, centers1, W1, b1
                 load_h(5)
             if s == 3:
                 load_h(6)
-            if s == 7:
+            if s == 5:
                 load_h(7)
             pool_some(POOL_PER_SLOT)
 
@@ -484,10 +540,13 @@ def tile_hierarchicalclustering_pa_t_kernel(tc, task_embedding, centers1, W1, b1
                 nc.vector.tensor_copy(out=ot[:], in_=accs[a][:])
             nc.sync.dma_start(out=out_view[:, a, :], in_=ot[:])
 
-        d_scalar(NG - 1, 768, 256)
+        v_r_tile(NG - 1, 2)
+        s_norm(NG - 1, 2, 0, 1024)
+        v_r_tile(NG - 1, 3)
+        s_norm(NG - 1, 3, 512, 512)
+        v_norm(NG - 1, 3, 0, 512)
         for q in range(4):
-            if q < 3:
-                d_piece(nc.vector, NG - 1, q * 256, 256)
+            v_regroup(NG - 1, q * 256, 256)
             v_qp(NG - 1, q * 256, 256)
             mark_p(NG - 1, 2 * q, 2 * q + 2)
             pool_some(100)

@@ -22,8 +22,6 @@ NARROW = 28
 POOL_PER_SLOT = 6
 DV = 0
 DS = 0
-DV_LATE = 1
-DS_LATE = 1
 
 
 def tile_hierarchicalclustering_pa_t_kernel(tc, task_embedding, centers1, W1, b1, out):
@@ -71,7 +69,6 @@ def tile_hierarchicalclustering_pa_t_kernel(tc, task_embedding, centers1, W1, b1
         sms = {}
         rinvs = {}
         pgrps = {}
-        pns = {}
 
         def load_h(g):
             hraw[g] = hpool.tile([P, 2048], BF16, tag="hraw", name="hraw%d" % g)
@@ -172,10 +169,7 @@ def tile_hierarchicalclustering_pa_t_kernel(tc, task_embedding, centers1, W1, b1
                     out=ses[g][:, t, hf * 512 : (hf + 1) * 512], in0=gps[(s, hf)][:], scalar=-0.5,
                     in1=c4b[:, hf * 512 : (hf + 1) * 512], op0=ALU.mult, op1=ALU.add,
                 )
-            if s >= NARROW:
-                nc.vector.tensor_reduce(out=mns[g][:, t : t + 1], in_=ses[g][:, t, :], axis=AX.X, op=ALU.min)
-            elif t % 2 == 1:
-                nc.vector.tensor_reduce(out=mns[g][:, t - 1 : t + 1], in_=ses[g][:, t - 1 : t + 1, :], axis=AX.X, op=ALU.min)
+            nc.vector.tensor_reduce(out=mns[g][:, t : t + 1], in_=ses[g][:, t, :], axis=AX.X, op=ALU.min)
 
         def s_c(s):
             g, t = divmod(s, 4)
@@ -199,40 +193,12 @@ def tile_hierarchicalclustering_pa_t_kernel(tc, task_embedding, centers1, W1, b1
                 op=ALU.mult,
             )
 
-        def d_scalar_t(g, lo, n, t):
-            nc.scalar.activation(
-                out=pgrps[g][:, lo : lo + n, t], in_=ses[g][:, t, lo : lo + n], func=ACT.Copy,
-                scale=rinvs[g][:, t : t + 1],
-            )
-
         def d_scalar(g, lo, n):
             for t in range(4):
-                d_scalar_t(g, lo, n, t)
-
-        def v_r_tile(g, t):
-            if t == 0:
-                rinvs[g] = small.tile([P, 4], F32, tag="rinv", name="rinv%d" % g)
-                pns[g] = grp.tile([P, 4, 1024], BF16, tag="pn", name="pn%d" % g, bufs=1)
-                pgrps[g] = grp.tile([P, 1024, 4], BF16, tag="pgrp", name="pgrp%d" % g, align_bytes=64)
-            nc.vector.reciprocal(rinvs[g][:, t : t + 1], sms[g][:, t : t + 1])
-
-        def s_norm(g, t, lo, n):
-            nc.scalar.activation(
-                out=pns[g][:, t, lo : lo + n], in_=ses[g][:, t, lo : lo + n], func=ACT.Copy,
-                scale=rinvs[g][:, t : t + 1],
-            )
-
-        def v_norm(g, t, lo, n):
-            nc.vector.tensor_scalar(
-                out=pns[g][:, t, lo : lo + n], in0=ses[g][:, t, lo : lo + n], scalar1=rinvs[g][:, t : t + 1],
-                scalar2=None, op0=ALU.mult,
-            )
-
-        def v_regroup(g, lo, n):
-            nc.vector.tensor_copy(
-                out=pgrps[g][:, lo : lo + n, :].rearrange("p (c i) t -> p c t i", i=4),
-                in_=pns[g][:, :, lo : lo + n].rearrange("p t (c i) -> p c t i", i=4),
-            )
+                nc.scalar.activation(
+                    out=pgrps[g][:, lo : lo + n, t], in_=ses[g][:, t, lo : lo + n], func=ACT.Copy,
+                    scale=rinvs[g][:, t : t + 1],
+                )
 
         def v_qp(g, lo, n):
             nc.vector.quantize_mx(
@@ -400,35 +366,28 @@ def tile_hierarchicalclustering_pa_t_kernel(tc, task_embedding, centers1, W1, b1
 
         units = []
 
-        h_ready = {0}
-
-        def qh_and_mark(g):
-            v_qh(g)
-            h_ready.add(g)
-
         def add_t(g):
-            units.append((lambda b: pe_t(g, 0, b), lambda: s_t(g, 0), None, None))
-            units.append((lambda b: pe_t(g, 1, b), lambda: s_t(g, 1), lambda: qh_and_mark(g), None))
+            units.append((lambda b: pe_t(g, 0, b), lambda: s_t(g, 0), None))
+            units.append((lambda b: pe_t(g, 1, b), lambda: s_t(g, 1), lambda: v_qh(g)))
 
         def add_z(g, d0):
-            units.append((lambda b: pe_z(g, d0, b), lambda: s_z(g, d0), None, g))
-            units.append((lambda b: pe_z(g, d0 + 1, b), lambda: s_z(g, d0 + 1), None, g))
+            units.append((lambda b: pe_z(g, d0, b), lambda: s_z(g, d0), None))
+            units.append((lambda b: pe_z(g, d0 + 1, b), lambda: s_z(g, d0 + 1), None))
 
         def qt_and_mark(g):
             v_qt(g)
             ready["t"] = g + 1
 
         def add_x(g):
-            units.append((lambda b: pe_x(g, 0, b), lambda: s_x(g, 0), None, None))
-            units.append((lambda b: pe_x(g, 1, b), lambda: s_x(g, 1), lambda: qt_and_mark(g), None))
+            units.append((lambda b: pe_x(g, 0, b), lambda: s_x(g, 0), None))
+            units.append((lambda b: pe_x(g, 1, b), lambda: s_x(g, 1), lambda: qt_and_mark(g)))
 
         add_t(1)
         add_z(0, 0)
         add_z(0, 2)
-        add_t(2)
         for gam in range(1, NG):
-            if gam + 2 < NG:
-                add_t(gam + 2)
+            if gam + 1 < NG:
+                add_t(gam + 1)
             add_x(gam - 1)
             add_z(gam, 0)
             add_z(gam, 2)
@@ -439,7 +398,7 @@ def tile_hierarchicalclustering_pa_t_kernel(tc, task_embedding, centers1, W1, b1
 
         def pe_pair(n=2):
             for i in range(n):
-                if state["pe"] < len(units) and (units[state["pe"]][3] is None or units[state["pe"]][3] in h_ready):
+                if state["pe"] < len(units):
                     units[state["pe"]][0](5 - (state["pe"] % 2))
                     state["pe"] += 1
 
@@ -456,24 +415,16 @@ def tile_hierarchicalclustering_pa_t_kernel(tc, task_embedding, centers1, W1, b1
                 vq[state["v"]]()
                 state["v"] += 1
 
-        def ds_of(g):
-            return DS_LATE if g == NG - 2 else DS
-
-        def dv_of(g):
-            return DV_LATE if g == NG - 3 else DV
-
-        def g_n(g):
-            return 1024 - (dv_of(g) + ds_of(g)) * P
+        G_N = 1024 - (DV + DS) * P
 
         def window(g):
             if g >= 2:
-                if dv_of(g - 2) > 0:
-                    d_piece(nc.vector, g - 2, 1024 - dv_of(g - 2) * P, dv_of(g - 2) * P)
+                if DV > 0:
+                    d_piece(nc.vector, g - 2, 1024 - DV * P, DV * P)
                 v_qp(g - 2, 0, 1024)
                 mark_p(g - 2, 0, NA)
             v_pending()
-            if g < NG:
-                v_r(g - 1)
+            v_r(g - 1)
 
         open_acc(0, 6)
         open_acc(1, 7)
@@ -483,19 +434,14 @@ def tile_hierarchicalclustering_pa_t_kernel(tc, task_embedding, centers1, W1, b1
             g, t = divmod(s, 4)
             if s > 0:
                 v_ab(s)
-            if s > NARROW:
-                s_c(s - 1)
-            elif t % 2 == 0 and s > 0:
-                s_c(s - 2)
                 s_c(s - 1)
             if g == 0:
                 v_pending()
-            elif (t == 1 and g < NG - 1) or (t == 0 and g == NG - 1):
+            elif t == 0:
                 window(g)
-                d_piece(nc.gpsimd, g - 1, 0, g_n(g - 1) // 2)
-                d_piece(nc.gpsimd, g - 1, g_n(g - 1) // 2, g_n(g - 1) // 2)
-                if ds_of(g - 1) > 0:
-                    d_scalar(g - 1, g_n(g - 1), ds_of(g - 1) * P)
+                d_piece(nc.gpsimd, g - 1, 0, G_N)
+                if DS > 0:
+                    d_scalar(g - 1, G_N, DS * P)
             if s + 2 <= NARROW:
                 pe_g(s + 2)
             elif s == NARROW - 1:
@@ -506,11 +452,8 @@ def tile_hierarchicalclustering_pa_t_kernel(tc, task_embedding, centers1, W1, b1
             else:
                 open_acc(6, 0)
                 open_acc(7, 1)
-            if s > NARROW + 1:
-                v_r_tile(NG - 1, t - 2)
-                s_norm(NG - 1, t - 2, 0, 1024)
             s_pair(3)
-            pe_pair(3 if t == 1 and g >= 1 else 2)
+            pe_pair(3 if t == 0 and g >= 1 else 2)
             if state["s"] == len(units) and 2 not in accs:
                 open_acc(2, 4)
                 open_acc(3, 5)
@@ -519,7 +462,7 @@ def tile_hierarchicalclustering_pa_t_kernel(tc, task_embedding, centers1, W1, b1
                 load_h(5)
             if s == 3:
                 load_h(6)
-            if s == 5:
+            if s == 7:
                 load_h(7)
             pool_some(POOL_PER_SLOT)
 
@@ -540,13 +483,10 @@ def tile_hierarchicalclustering_pa_t_kernel(tc, task_embedding, centers1, W1, b1
                 nc.vector.tensor_copy(out=ot[:], in_=accs[a][:])
             nc.sync.dma_start(out=out_view[:, a, :], in_=ot[:])
 
-        v_r_tile(NG - 1, 2)
-        s_norm(NG - 1, 2, 0, 1024)
-        v_r_tile(NG - 1, 3)
-        s_norm(NG - 1, 3, 512, 512)
-        v_norm(NG - 1, 3, 0, 512)
+        d_scalar(NG - 1, 768, 256)
         for q in range(4):
-            v_regroup(NG - 1, q * 256, 256)
+            if q < 3:
+                d_piece(nc.vector, NG - 1, q * 256, 256)
             v_qp(NG - 1, q * 256, 256)
             mark_p(NG - 1, 2 * q, 2 * q + 2)
             pool_some(100)

@@ -193,12 +193,15 @@ def tile_hierarchicalclustering_pa_t_kernel(tc, task_embedding, centers1, W1, b1
                 op=ALU.mult,
             )
 
+        def d_scalar_t(g, lo, n, t):
+            nc.scalar.activation(
+                out=pgrps[g][:, lo : lo + n, t], in_=ses[g][:, t, lo : lo + n], func=ACT.Copy,
+                scale=rinvs[g][:, t : t + 1],
+            )
+
         def d_scalar(g, lo, n):
             for t in range(4):
-                nc.scalar.activation(
-                    out=pgrps[g][:, lo : lo + n, t], in_=ses[g][:, t, lo : lo + n], func=ACT.Copy,
-                    scale=rinvs[g][:, t : t + 1],
-                )
+                d_scalar_t(g, lo, n, t)
 
         def v_qp(g, lo, n):
             nc.vector.quantize_mx(
@@ -439,7 +442,7 @@ def tile_hierarchicalclustering_pa_t_kernel(tc, task_embedding, centers1, W1, b1
                 v_pending()
             elif t == 0:
                 window(g)
-                d_piece(nc.gpsimd, g - 1, 0, G_N)
+                d_piece(nc.gpsimd, g - 1, 0, 768 if g == NG - 1 else G_N)
                 if DS > 0:
                     d_scalar(g - 1, G_N, DS * P)
             if s + 2 <= NARROW:
@@ -453,6 +456,8 @@ def tile_hierarchicalclustering_pa_t_kernel(tc, task_embedding, centers1, W1, b1
                 open_acc(6, 0)
                 open_acc(7, 1)
             s_pair(3)
+            if g == NG - 1:
+                d_scalar_t(g - 1, 768, 256, t)
             pe_pair(3 if t == 0 and g >= 1 else 2)
             if state["s"] == len(units) and 2 not in accs:
                 open_acc(2, 4)

@@ -110,27 +110,28 @@ def tile_hierarchicalclustering_pa_t_kernel(tc, task_embedding, centers1, W1, b1
 
         def s_z(g, dt):
             if dt == 0:
-                tTs[g] = grp.tile([P, 4, 512], BF16, tag="tT", name="tT%d" % g)
+                tTs[g] = grp.tile([P, 4, 2, P, 2], BF16, tag="tT", name="tT%d" % g)
             nc.scalar.activation(
-                out=tTs[g][:, dt, :], in_=xbanks[("z", g, dt)][:], func=ACT.Tanh,
-                bias=b1c[:, dt : dt + 1], scale=1.0,
+                out=tTs[g][:, dt, :, :, :],
+                in_=xbanks[("z", g, dt)][:].rearrange("d (u e p) -> d u p e", u=2, e=2),
+                func=ACT.Tanh, bias=b1c[:, dt : dt + 1], scale=1.0,
             )
 
         def pe_x(g, hb, b):
-            xt = bank(b, [P, 4, 256], BF16, "xt%d_%d" % (g, hb))
+            xt = bank(b, [P, 2, 256], F32, "xt%d_%d" % (g, hb))
+            words = tTs[g][:].rearrange("d a u p e -> d (a u p e)").bitcast(F32)
             for dl in range(2):
-                for t in range(4):
-                    nc.tensor.transpose(
-                        xt[:, t, dl * P : (dl + 1) * P], tTs[g][:, 2 * hb + dl, t * P : (t + 1) * P], ident_b[:]
-                    )
+                for u in range(2):
+                    lo = (2 * hb + dl) * 256 + u * P
+                    nc.tensor.transpose(xt[:, u, dl * P : (dl + 1) * P], words[:, lo : lo + P], ident_f[:])
             xbanks[("x", g, hb)] = xt
 
         def s_x(g, hb):
             if hb == 0:
                 tgrps[g] = grp.tile([P, 512, 4], BF16, tag="tgrp", name="tgrp%d" % g, align_bytes=64)
             nc.scalar.copy(
-                out=tgrps[g][:, hb * 256 : (hb + 1) * 256, :],
-                in_=xbanks[("x", g, hb)][:].rearrange("p t d -> p d t"),
+                out=tgrps[g][:, hb * 256 : (hb + 1) * 256, :].bitcast(F32),
+                in_=xbanks[("x", g, hb)][:].rearrange("p u d -> p d u"),
             )
 
         def v_qt(g):

@@ -18,7 +18,9 @@ P = 128
 NG = 8
 NA = 8
 NS = 32
-NARROW = 28
+WIN = 1
+G_LAST = 768
+LAST_SHARE = {2: (0, 1), 3: (2, 3)}
 POOL_PER_SLOT = 6
 DV = 0
 DS = 0
@@ -140,36 +142,32 @@ def tile_hierarchicalclustering_pa_t_kernel(tc, task_embedding, centers1, W1, b1
                 in_=tgrps[g][:].rearrange("p d t -> p (d t)"),
             )
 
-        def g_banks(s):
-            if s >= NARROW:
-                return (0, 1)
-            return ((2 * s) % 4, (2 * s) % 4 + 1)
-
-        def pe_g(s):
+        def pe_g(s, hf):
             g, t = divmod(s, 4)
-            for hf in range(2):
-                gp = bank(g_banks(s)[hf], [P, 512], F32, "gp%d_%d" % (s, hf))
-                nc.tensor.matmul_mx(
-                    out=gp[:],
-                    lhsT=hc[:, g, t * P : (t + 1) * P].bitcast(FP8X4),
-                    lhsT_scale=hs[:, g, t * P : (t + 1) * P],
-                    rhs=cc[:, hf * 512 : (hf + 1) * 512].bitcast(FP8X4),
-                    rhs_scale=cs[:, hf * 512 : (hf + 1) * 512],
-                    start=True,
-                    stop=True,
-                )
-                gps[(s, hf)] = gp
+            gp = bank(hf, [P, 512], F32, "gp%d_%d" % (s, hf))
+            nc.tensor.matmul_mx(
+                out=gp[:],
+                lhsT=hc[:, g, t * P : (t + 1) * P].bitcast(FP8X4),
+                lhsT_scale=hs[:, g, t * P : (t + 1) * P],
+                rhs=cc[:, hf * 512 : (hf + 1) * 512].bitcast(FP8X4),
+                rhs_scale=cs[:, hf * 512 : (hf + 1) * 512],
+                start=True,
+                stop=True,
+            )
+            gps[(s, hf)] = gp
 
-        def v_ab(s):
+        def v_a(s, hf):
             g, t = divmod(s, 4)
-            if t == 0:
+            if t == 0 and hf == 0:
                 ses[g] = spool.tile([P, 4, 1024], F32, tag="se", name="se%d" % g)
                 mns[g] = small.tile([P, 4], F32, tag="mn", name="mn%d" % g)
-            for hf in range(2):
-                nc.vector.scalar_tensor_tensor(
-                    out=ses[g][:, t, hf * 512 : (hf + 1) * 512], in0=gps[(s, hf)][:], scalar=-0.5,
-                    in1=c4b[:, hf * 512 : (hf + 1) * 512], op0=ALU.mult, op1=ALU.add,
-                )
+            nc.vector.scalar_tensor_tensor(
+                out=ses[g][:, t, hf * 512 : (hf + 1) * 512], in0=gps[(s, hf)][:], scalar=-0.5,
+                in1=c4b[:, hf * 512 : (hf + 1) * 512], op0=ALU.mult, op1=ALU.add,
+            )
+
+        def v_b(s):
+            g, t = divmod(s, 4)
             nc.vector.tensor_reduce(out=mns[g][:, t : t + 1], in_=ses[g][:, t, :], axis=AX.X, op=ALU.min)
 
         def s_c(s):
@@ -349,8 +347,8 @@ def tile_hierarchicalclustering_pa_t_kernel(tc, task_embedding, centers1, W1, b1
                         lo = (2 * pair + al) * 256 + u * 128
                         nc.tensor.transpose(xw[:, al, u, :], ww[:, lo : lo + 128], ident_f[:])
                 xws.append(xw)
-            pe_g(0)
-            pe_g(1)
+            pe_g(0, 0)
+            pe_g(0, 1)
             for pair in range(2):
                 nc.scalar.copy(
                     out=wgw[:, 2 * pair : 2 * pair + 2, :, :], in_=xws[pair][:].rearrange("q a u j -> q a j u")
@@ -362,7 +360,6 @@ def tile_hierarchicalclustering_pa_t_kernel(tc, task_embedding, centers1, W1, b1
             def v_qw():
                 nc.vector.quantize_mx(out=wc[:].bitcast(FP8X4), scales=ws[:], in_=wgrp[:])
 
-            v_ab(0)
             v_qw()
 
         grp = ctx.enter_context(tc.tile_pool(name="grp", bufs=2))
@@ -403,7 +400,7 @@ def tile_hierarchicalclustering_pa_t_kernel(tc, task_embedding, centers1, W1, b1
         def pe_pair(n=2):
             for i in range(n):
                 if state["pe"] < len(units):
-                    units[state["pe"]][0](5 - (state["pe"] % 2))
+                    units[state["pe"]][0](2 + state["pe"] % 4)
                     state["pe"] += 1
 
         def s_pair(n=2):
@@ -436,33 +433,31 @@ def tile_hierarchicalclustering_pa_t_kernel(tc, task_embedding, centers1, W1, b1
         pe_pair()
         for s in range(NS):
             g, t = divmod(s, 4)
+            v_a(s, 0)
+            if s + 1 < NS:
+                pe_g(s + 1, 0)
             if s > 0:
-                v_ab(s)
-                s_c(s - 1)
+                v_b(s - 1)
+            v_a(s, 1)
+            if s + 1 < NS:
+                pe_g(s + 1, 1)
             if g == 0:
                 v_pending()
-            elif t == 0:
+            elif t == WIN:
                 window(g)
-                d_piece(nc.gpsimd, g - 1, 0, 768 if g == NG - 1 else G_N)
+                d_piece(nc.gpsimd, g - 1, 0, G_LAST if g == NG - 1 else G_N)
                 if DS > 0:
                     d_scalar(g - 1, G_N, DS * P)
-            if s + 2 <= NARROW:
-                pe_g(s + 2)
-            elif s == NARROW - 1:
-                open_acc(4, 2)
-                open_acc(5, 3)
-            elif s + 1 < NS:
-                pe_g(s + 1)
-            else:
-                open_acc(6, 0)
-                open_acc(7, 1)
             s_pair(3)
-            if g == NG - 1:
-                d_scalar_t(g - 1, 768, 256, t)
-            pe_pair(3 if t == 0 and g >= 1 else 2)
+            if g == NG - 1 and t >= 2:
+                for i in LAST_SHARE[t]:
+                    d_scalar_t(g - 1, G_LAST, 1024 - G_LAST, i)
+            if s > 0:
+                s_c(s - 1)
+            pe_pair(3 if t == 0 and 1 <= g <= 4 else 2)
             if state["s"] == len(units) and 2 not in accs:
-                open_acc(2, 4)
-                open_acc(3, 5)
+                for a in range(2, 6):
+                    open_acc(a, a)
             if s == 0:
                 load_h(4)
                 load_h(5)
@@ -472,29 +467,38 @@ def tile_hierarchicalclustering_pa_t_kernel(tc, task_embedding, centers1, W1, b1
                 load_h(7)
             pool_some(POOL_PER_SLOT)
 
+        v_b(NS - 1)
         s_c(NS - 1)
-        s_pair(100)
-        if 2 not in accs:
-            open_acc(2, 4)
-            open_acc(3, 5)
+        open_acc(6, 0)
+        open_acc(7, 1)
         pool_some(100)
-        window(NG)
+        v_qp(NG - 2, 0, 1024)
+        mark_p(NG - 2, 0, NA)
         pool_some(100)
+        v_r(NG - 1)
 
         def finish(a):
             ot = ostage.tile([P, 512], F32, tag="ot", name="ot%d" % a)
-            if a < NA - 1:
-                nc.scalar.copy(out=ot[:], in_=accs[a][:])
-            else:
+            if a in (5, 7):
                 nc.vector.tensor_copy(out=ot[:], in_=accs[a][:])
+            else:
+                nc.scalar.copy(out=ot[:], in_=accs[a][:])
             nc.sync.dma_start(out=out_view[:, a, :], in_=ot[:])
 
-        d_scalar(NG - 1, 768, 256)
-        for q in range(4):
-            if q < 3:
-                d_piece(nc.vector, NG - 1, q * 256, 256)
+        def quarter(q):
             v_qp(NG - 1, q * 256, 256)
             mark_p(NG - 1, 2 * q, 2 * q + 2)
             pool_some(100)
-            finish(2 * q)
-            finish(2 * q + 1)
+
+        d_scalar(NG - 1, 768, 256)
+        d_piece(nc.vector, NG - 1, 0, 256)
+        d_piece(nc.vector, NG - 1, 256, 256)
+        quarter(0)
+        d_piece(nc.vector, NG - 1, 512, 256)
+        quarter(1)
+        for a in range(4):
+            finish(a)
+        quarter(3)
+        quarter(2)
+        for a in (6, 7, 4, 5):
+            finish(a)

@@ -19,11 +19,10 @@ NG = 8
 NA = 8
 NS = 32
 WIN = 1
+SIDE = 3
 G_LAST = 768
 LAST_SHARE = {2: (0, 1), 3: (2, 3)}
 POOL_PER_SLOT = 6
-DV = 0
-DS = 0
 
 
 def tile_hierarchicalclustering_pa_t_kernel(tc, task_embedding, centers1, W1, b1, out):
@@ -240,130 +239,15 @@ def tile_hierarchicalclustering_pa_t_kernel(tc, task_embedding, centers1, W1, b1
             for a in range(a_lo, a_hi):
                 ready["p"][a] = g + 1
 
-        make_identity(nc, ident_f[:])
-        with tc.tile_pool(name="head", bufs=1) as head:
-            b1rows = head.tile([P, P], BF16)
-            nc.gpsimd.memset(b1rows[:], 0.0)
-            make_identity(nc, ident_b[:])
-            c_sb = head.tile([P, NA, 512], BF16)
-            for k in range(4):
-                nc.sync.dma_start(out=c_sb[:, 2 * k : 2 * k + 2, :], in_=c_view[:, 2 * k : 2 * k + 2, :])
-            load_h(0)
-            w_sb = head.tile([P, 4, 512], BF16)
-            nc.sync.dma_start(out=w_sb[:], in_=w_view)
-            nc.sync.dma_start(out=b1rows[0:4, :], in_=b1.rearrange("(a p) -> a p", p=P))
-            load_h(1)
-            load_h(2)
-            load_h(3)
-
-            cw = c_sb[:].rearrange("p a k -> p (a k)").bitcast(F32)
-            cgrp = head.tile([P, 4096], BF16, align_bytes=64)
-            cgw = cgrp[:].bitcast(F32).rearrange("q (a j u) -> q a j u", a=NA, u=2)
-            csq_s = head.tile([P, 4], F32)
-            csq_v = head.tile([P, 4], F32)
-            junk_s = head.tile([P, 512], F32)
-            junk_v = head.tile([P, 512], F32)
-            rep = head.tile([P, 4, 2, P], F32)
-            xcs = []
-            xrs = []
-
-            def pe_c(k):
-                xc = bank(k, [P, 2, 2, P], F32, "xc%d" % k)
-                for al in range(2):
-                    for u in range(2):
-                        lo = (2 * k + al) * 256 + u * 128
-                        nc.tensor.transpose(xc[:, al, u, :], cw[:, lo : lo + 128], ident_f[:])
-                xcs.append(xc)
-
-            def csq(k):
-                nc.scalar.activation(
-                    out=junk_s[:], in_=c_sb[:, 2 * k, :], func=ACT.Square, accum_out=csq_s[:, k : k + 1]
-                )
-                nc.vector.scalar_tensor_tensor(
-                    out=junk_v[:], in0=c_sb[:, 2 * k + 1, :], scalar=1.0, in1=c_sb[:, 2 * k + 1, :],
-                    op0=ALU.mult, op1=ALU.mult, accum_out=csq_v[:, k : k + 1],
-                )
-
-            def v_rep(hf):
-                for par, src in ((0, csq_s), (1, csq_v)):
-                    nc.gpsimd.tensor_scalar(
-                        out=rep[:, 2 * hf : 2 * hf + 2, par, :],
-                        in0=src[:, 2 * hf : 2 * hf + 2].unsqueeze(2).to_broadcast([P, 2, P]),
-                        scalar1=0.25, scalar2=0.0, op0=ALU.mult, op1=ALU.add,
-                    )
-
-            def pe_rep(hf):
-                xr = bank(6 + hf, [P, 4, P], F32, "xr%d" % hf)
-                for al in range(4):
-                    nc.tensor.transpose(xr[:, al, :], rep[:, 2 * hf + al // 2, al % 2, :], ident_f[:])
-                xrs.append(xr)
-
-            def c_evac(eng_copy, k):
-                eng_copy(out=cgw[:, 2 * k : 2 * k + 2, :, :], in_=xcs[k][:].rearrange("q a u j -> q a j u"))
-
-            def c4b_evac(eng_copy, hf):
-                eng_copy(out=c4b[:, hf * 512 : (hf + 1) * 512], in_=xrs[hf][:].rearrange("p a j -> p (a j)"))
-
-            def v_qc(hf):
-                nc.vector.quantize_mx(
-                    out=cc[:, hf * 512 : (hf + 1) * 512].bitcast(FP8X4), scales=cs[:, hf * 512 : (hf + 1) * 512],
-                    in_=cgrp[:, hf * 2048 : (hf + 1) * 2048],
-                )
-
-            pe_c(0)
-            csq(0)
-            pe_c(1)
-            csq(1)
-            v_rep(0)
-            pe_c(2)
-            csq(2)
-            pe_rep(0)
-            pe_c(3)
-            csq(3)
-            v_rep(1)
-            pe_t(0, 0, 4)
-            pe_t(0, 1, 5)
-            pe_rep(1)
-            c_evac(nc.scalar.copy, 0)
-            c_evac(nc.scalar.copy, 1)
-            c_evac(nc.vector.tensor_copy, 2)
-            c_evac(nc.vector.tensor_copy, 3)
-            v_qc(0)
-            c4b_evac(nc.vector.tensor_copy, 0)
-            s_t(0, 0)
-            s_t(0, 1)
-            v_qh(0)
-            c4b_evac(nc.scalar.copy, 1)
-            v_qc(1)
-
-            ww = w_sb[:].rearrange("p a k -> p (a k)").bitcast(F32)
-            wgrp = head.tile([P, 2048], BF16, align_bytes=64)
-            wgw = wgrp[:].bitcast(F32).rearrange("q (a j u) -> q a j u", a=4, u=2)
-            xws = []
-            for pair in range(2):
-                xw = bank(4 + pair, [P, 2, 2, P], F32, "xw%d" % pair)
-                for al in range(2):
-                    for u in range(2):
-                        lo = (2 * pair + al) * 256 + u * 128
-                        nc.tensor.transpose(xw[:, al, u, :], ww[:, lo : lo + 128], ident_f[:])
-                xws.append(xw)
-            pe_g(0, 0)
-            pe_g(0, 1)
-            for pair in range(2):
-                nc.scalar.copy(
-                    out=wgw[:, 2 * pair : 2 * pair + 2, :, :], in_=xws[pair][:].rearrange("q a u j -> q a j u")
-                )
-            xb = bank(4, [P, P], BF16, "xb")
-            nc.tensor.transpose(xb[:], b1rows[:], ident_b[:])
-            nc.scalar.copy(out=b1c[:], in_=xb[:, 0:4])
-
-            def v_qw():
-                nc.vector.quantize_mx(out=wc[:].bitcast(FP8X4), scales=ws[:], in_=wgrp[:])
-
-            v_qw()
-
-        grp = ctx.enter_context(tc.tile_pool(name="grp", bufs=2))
-        ostage = ctx.enter_context(tc.tile_pool(name="ostage", bufs=8))
+        def scores(s):
+            v_a(s, 0)
+            if s + 1 < NS:
+                pe_g(s + 1, 0)
+            if s > 0:
+                v_b(s - 1)
+            v_a(s, 1)
+            if s + 1 < NS:
+                pe_g(s + 1, 1)
 
         units = []
 
@@ -400,7 +284,7 @@ def tile_hierarchicalclustering_pa_t_kernel(tc, task_embedding, centers1, W1, b1
         def pe_pair(n=2):
             for i in range(n):
                 if state["pe"] < len(units):
-                    units[state["pe"]][0](2 + state["pe"] % 4)
+                    units[state["pe"]][0](2 + state["pe"] % SIDE)
                     state["pe"] += 1
 
         def s_pair(n=2):
@@ -416,38 +300,176 @@ def tile_hierarchicalclustering_pa_t_kernel(tc, task_embedding, centers1, W1, b1
                 vq[state["v"]]()
                 state["v"] += 1
 
-        G_N = 1024 - (DV + DS) * P
+        make_identity(nc, ident_f[:])
+        with tc.tile_pool(name="head", bufs=1) as head:
+            b1rows = head.tile([P, P], BF16)
+            nc.gpsimd.memset(b1rows[:], 0.0)
+            make_identity(nc, ident_b[:])
+            c_sb = head.tile([P, NA, 512], BF16)
+
+            def load_c(k):
+                nc.sync.dma_start(out=c_sb[:, 2 * k : 2 * k + 2, :], in_=c_view[:, 2 * k : 2 * k + 2, :])
+
+            load_c(0)
+            load_c(1)
+            load_h(0)
+            load_c(2)
+            load_c(3)
+            w_sb = head.tile([P, 4, 512], BF16)
+            nc.sync.dma_start(out=w_sb[:], in_=w_view)
+            nc.sync.dma_start(out=b1rows[0:4, :], in_=b1.rearrange("(a p) -> a p", p=P))
+            load_h(1)
+            load_h(2)
+            load_h(3)
+
+            cw = c_sb[:].rearrange("p a k -> p (a k)").bitcast(F32)
+            cgrp = head.tile([P, 4096], BF16, align_bytes=64)
+            cgw = cgrp[:].bitcast(F32).rearrange("q (a j u) -> q a j u", a=NA, u=2)
+            csq_s = head.tile([P, NA], F32)
+            csq_v = head.tile([P, NA], F32)
+            junk_s = head.tile([P, 512], F32)
+            junk_v = head.tile([P, 512], F32)
+            csqs = {}
+            xcs = {}
+            xrs = {}
+            xws = {}
+
+            def pe_c(k):
+                xcs[k] = bank(k, [P, 2, 2, P], F32, "xc%d" % k)
+                for al in range(2):
+                    for u in range(2):
+                        lo = (2 * k + al) * 256 + u * 128
+                        nc.tensor.transpose(xcs[k][:, al, u, :], cw[:, lo : lo + 128], ident_f[:])
+
+            def csq_scalar(a):
+                nc.scalar.activation(
+                    out=junk_s[:], in_=c_sb[:, a, :], func=ACT.Square, accum_out=csq_s[:, a : a + 1]
+                )
+                csqs[a] = csq_s
+
+            def csq_vector(a):
+                nc.vector.scalar_tensor_tensor(
+                    out=junk_v[:], in0=c_sb[:, a, :], scalar=1.0, in1=c_sb[:, a, :],
+                    op0=ALU.mult, op1=ALU.mult, accum_out=csq_v[:, a : a + 1],
+                )
+                csqs[a] = csq_v
+
+            def pe_rep(hf):
+                xrs[hf] = bank(6 + hf, [P, 4, P], F32, "xr%d" % hf)
+                for al in range(4):
+                    a = 4 * hf + al
+                    nc.tensor.transpose(xrs[hf][:, al, :], csqs[a][:, a : a + 1].to_broadcast([P, P]), ident_f[:])
+
+            def c_evac(eng_copy, k):
+                eng_copy(out=cgw[:, 2 * k : 2 * k + 2, :, :], in_=xcs[k][:].rearrange("q a u j -> q a j u"))
+
+            def c4b_scalar(hf):
+                nc.scalar.activation(
+                    out=c4b[:, hf * 512 : (hf + 1) * 512], in_=xrs[hf][:].rearrange("p a j -> p (a j)"),
+                    func=ACT.Copy, scale=0.25,
+                )
+
+            def c4b_vector(hf):
+                nc.vector.tensor_scalar_mul(
+                    c4b[:, hf * 512 : (hf + 1) * 512], xrs[hf][:].rearrange("p a j -> p (a j)"), 0.25
+                )
+
+            def v_qc(hf):
+                nc.vector.quantize_mx(
+                    out=cc[:, hf * 512 : (hf + 1) * 512].bitcast(FP8X4), scales=cs[:, hf * 512 : (hf + 1) * 512],
+                    in_=cgrp[:, hf * 2048 : (hf + 1) * 2048],
+                )
+
+            ww = w_sb[:].rearrange("p a k -> p (a k)").bitcast(F32)
+            wgrp = head.tile([P, 2048], BF16, align_bytes=64)
+            wgw = wgrp[:].bitcast(F32).rearrange("q (a j u) -> q a j u", a=4, u=2)
+
+            def pe_w(pair, b):
+                xws[pair] = bank(b, [P, 2, 2, P], F32, "xw%d" % pair)
+                for al in range(2):
+                    for u in range(2):
+                        lo = (2 * pair + al) * 256 + u * 128
+                        nc.tensor.transpose(xws[pair][:, al, u, :], ww[:, lo : lo + 128], ident_f[:])
+
+            def s_w(pair):
+                nc.scalar.copy(
+                    out=wgw[:, 2 * pair : 2 * pair + 2, :, :], in_=xws[pair][:].rearrange("q a u j -> q a j u")
+                )
+
+            def pe_b1(b):
+                xws["b1"] = bank(b, [P, P], BF16, "xb")
+                nc.tensor.transpose(xws["b1"][:], b1rows[:], ident_b[:])
+
+            def s_b1():
+                nc.scalar.copy(out=b1c[:], in_=xws["b1"][:, 0:4])
+
+            def v_qw():
+                nc.vector.quantize_mx(out=wc[:].bitcast(FP8X4), scales=ws[:], in_=wgrp[:])
+
+            pe_c(0)
+            csq_scalar(0)
+            csq_vector(1)
+            pe_c(1)
+            csq_scalar(2)
+            csq_vector(3)
+            pe_t(0, 0, 4)
+            pe_t(0, 1, 5)
+            pe_c(2)
+            pe_c(3)
+            pe_rep(0)
+            c_evac(nc.scalar.copy, 0)
+            c_evac(nc.vector.tensor_copy, 1)
+            csq_scalar(4)
+            csq_vector(5)
+            v_qc(0)
+            s_t(0, 0)
+            s_t(0, 1)
+            c_evac(nc.vector.tensor_copy, 2)
+            csq_vector(7)
+            v_qh(0)
+            csq_scalar(6)
+            c4b_vector(0)
+            c_evac(nc.scalar.copy, 3)
+            pe_w(0, 4)
+            pe_w(1, 5)
+            pe_g(0, 0)
+            pe_rep(1)
+            v_qc(1)
+            v_a(0, 0)
+            s_w(0)
+            c4b_scalar(1)
+            s_w(1)
+            pe_g(0, 1)
+            pe_g(1, 0)
+            pe_pair()
+            pe_b1(6)
+            v_a(0, 1)
+            pe_g(1, 1)
+            s_b1()
+            v_qw()
+
+
+        grp = ctx.enter_context(tc.tile_pool(name="grp", bufs=2))
+        ostage = ctx.enter_context(tc.tile_pool(name="ostage", bufs=8))
 
         def window(g):
+            v_pending()
             if g >= 2:
-                if DV > 0:
-                    d_piece(nc.vector, g - 2, 1024 - DV * P, DV * P)
                 v_qp(g - 2, 0, 1024)
                 mark_p(g - 2, 0, NA)
-            v_pending()
             v_r(g - 1)
 
-        open_acc(0, 6)
-        open_acc(1, 7)
-
-        pe_pair()
+        for a in range(6 - SIDE):
+            open_acc(a, 2 + SIDE + a)
         for s in range(NS):
             g, t = divmod(s, 4)
-            v_a(s, 0)
-            if s + 1 < NS:
-                pe_g(s + 1, 0)
             if s > 0:
-                v_b(s - 1)
-            v_a(s, 1)
-            if s + 1 < NS:
-                pe_g(s + 1, 1)
+                scores(s)
             if g == 0:
                 v_pending()
             elif t == WIN:
                 window(g)
-                d_piece(nc.gpsimd, g - 1, 0, G_LAST if g == NG - 1 else G_N)
-                if DS > 0:
-                    d_scalar(g - 1, G_N, DS * P)
+                d_piece(nc.gpsimd, g - 1, 0, G_LAST if g == NG - 1 else 1024)
             s_pair(3)
             if g == NG - 1 and t >= 2:
                 for i in LAST_SHARE[t]:
@@ -455,9 +477,9 @@ def tile_hierarchicalclustering_pa_t_kernel(tc, task_embedding, centers1, W1, b1
             if s > 0:
                 s_c(s - 1)
             pe_pair(3 if t == 0 and 1 <= g <= 4 else 2)
-            if state["s"] == len(units) and 2 not in accs:
-                for a in range(2, 6):
-                    open_acc(a, a)
+            if state["s"] == len(units) and 5 not in accs:
+                for a in range(6 - SIDE, 6):
+                    open_acc(a, a + SIDE - 4)
             if s == 0:
                 load_h(4)
                 load_h(5)

@@ -295,8 +295,8 @@ def tile_hierarchicalclustering_pa_t_kernel(tc, task_embedding, centers1, W1, b1
                         vq.append(units[state["s"]][2])
                     state["s"] += 1
 
-        def v_pending():
-            while state["v"] < len(vq):
+        def v_pending(keep_back=0):
+            while state["v"] < len(vq) - keep_back:
                 vq[state["v"]]()
                 state["v"] += 1
 
@@ -453,11 +453,12 @@ def tile_hierarchicalclustering_pa_t_kernel(tc, task_embedding, centers1, W1, b1
         ostage = ctx.enter_context(tc.tile_pool(name="ostage", bufs=8))
 
         def window(g):
-            v_pending()
+            v_pending(1)
             if g >= 2:
                 v_qp(g - 2, 0, 1024)
                 mark_p(g - 2, 0, NA)
             v_r(g - 1)
+            v_pending()
 
         for a in range(6 - SIDE):
             open_acc(a, 2 + SIDE + a)
@@ -507,20 +508,25 @@ def tile_hierarchicalclustering_pa_t_kernel(tc, task_embedding, centers1, W1, b1
                 nc.scalar.copy(out=ot[:], in_=accs[a][:])
             nc.sync.dma_start(out=out_view[:, a, :], in_=ot[:])
 
-        def quarter(q):
-            v_qp(NG - 1, q * 256, 256)
-            mark_p(NG - 1, 2 * q, 2 * q + 2)
+        def quant(lo, n):
+            v_qp(NG - 1, lo, n)
+            mark_p(NG - 1, lo // P, (lo + n) // P)
             pool_some(100)
 
-        d_scalar(NG - 1, 768, 256)
+        d_scalar(NG - 1, 896, 128)
         d_piece(nc.vector, NG - 1, 0, 256)
+        quant(0, 256)
         d_piece(nc.vector, NG - 1, 256, 256)
-        quarter(0)
+        finish(0)
+        finish(1)
+        quant(256, 256)
         d_piece(nc.vector, NG - 1, 512, 256)
-        quarter(1)
-        for a in range(4):
-            finish(a)
-        quarter(3)
-        quarter(2)
-        for a in (6, 7, 4, 5):
-            finish(a)
+        finish(2)
+        finish(3)
+        quant(512, 256)
+        d_piece(nc.vector, NG - 1, 768, 128)
+        quant(768, 256)
+        finish(4)
+        finish(5)
+        finish(6)
+        finish(7)

@@ -514,19 +514,26 @@ def tile_hierarchicalclustering_pa_t_kernel(tc, task_embedding, centers1, W1, b1
             pool_some(100)
 
         d_scalar(NG - 1, 896, 128)
-        d_piece(nc.vector, NG - 1, 0, 256)
-        quant(0, 256)
-        d_piece(nc.vector, NG - 1, 256, 256)
+        d_piece(nc.vector, NG - 1, 0, 128)
+        d_piece(nc.vector, NG - 1, 128, 128)
+        quant(0, 128)
+        d_piece(nc.vector, NG - 1, 256, 128)
+        quant(128, 128)
         finish(0)
+        d_piece(nc.vector, NG - 1, 384, 128)
+        quant(256, 128)
         finish(1)
-        quant(256, 256)
-        d_piece(nc.vector, NG - 1, 512, 256)
+        d_piece(nc.vector, NG - 1, 512, 128)
+        quant(384, 128)
         finish(2)
+        d_piece(nc.vector, NG - 1, 640, 128)
+        quant(512, 128)
         finish(3)
-        quant(512, 256)
         d_piece(nc.vector, NG - 1, 768, 128)
-        quant(768, 256)
+        quant(640, 128)
         finish(4)
+        quant(768, 128)
         finish(5)
+        quant(896, 128)
         finish(6)
         finish(7)

@@ -302,6 +302,15 @@ def tile_hierarchicalclustering_pa_t_kernel(tc, task_embedding, centers1, W1, b1
 
         make_identity(nc, ident_f[:])
         with tc.tile_pool(name="head", bufs=1) as head:
+            zeros = head.tile([P, 512], BF16)
+            nc.vector.memset(zeros[:], 0.0)
+            idle = bank(7, [P, 512], F32, "idle")
+
+            def pe_warm(n):
+                for i in range(n):
+                    nc.tensor.matmul(idle[:], lhsT=zeros[:, 0:P], rhs=zeros[:], start=True, stop=True)
+
+            pe_warm(4)
             b1rows = head.tile([P, P], BF16)
             nc.gpsimd.memset(b1rows[:], 0.0)
             make_identity(nc, ident_b[:])
@@ -409,7 +418,9 @@ def tile_hierarchicalclustering_pa_t_kernel(tc, task_embedding, centers1, W1, b1
             pe_c(0)
             csq_scalar(0)
             csq_vector(1)
+            pe_warm(1)
             pe_c(1)
+            pe_warm(2)
             csq_scalar(2)
             csq_vector(3)
             pe_t(0, 0, 4)
@@ -417,6 +428,7 @@ def tile_hierarchicalclustering_pa_t_kernel(tc, task_embedding, centers1, W1, b1
             pe_c(2)
             pe_c(3)
             pe_rep(0)
+            pe_warm(2)
             c_evac(nc.scalar.copy, 0)
             c_evac(nc.vector.tensor_copy, 1)
             csq_scalar(4)
@@ -432,6 +444,7 @@ def tile_hierarchicalclustering_pa_t_kernel(tc, task_embedding, centers1, W1, b1
             c_evac(nc.scalar.copy, 3)
             pe_w(0, 4)
             pe_w(1, 5)
+            pe_warm(2)
             pe_g(0, 0)
             pe_rep(1)
             v_qc(1)

@@ -22,7 +22,7 @@ WIN = 1
 SIDE = 3
 G_LAST = 768
 LAST_SHARE = {2: (0, 1), 3: (2, 3)}
-POOL_PER_SLOT = 6
+POOL_PER_SLOT = 8
 
 
 def tile_hierarchicalclustering_pa_t_kernel(tc, task_embedding, centers1, W1, b1, out):
@@ -234,6 +234,11 @@ def tile_hierarchicalclustering_pa_t_kernel(tc, task_embedding, centers1, W1, b1
                 while n < limit and done[a] < min(ready["p"][a], ready["t"]):
                     pool_pass(a, done[a])
                     n += 1
+
+        def pool_upto(n):
+            for a in range(min(n, NA)):
+                while done[a] < min(ready["p"][a], ready["t"]):
+                    pool_pass(a, done[a])
 
         def mark_p(g, a_lo, a_hi):
             for a in range(a_lo, a_hi):
@@ -510,12 +515,12 @@ def tile_hierarchicalclustering_pa_t_kernel(tc, task_embedding, centers1, W1, b1
         pool_some(100)
         v_qp(NG - 2, 0, 1024)
         mark_p(NG - 2, 0, NA)
-        pool_some(100)
+        pool_upto(3)
         v_r(NG - 1)
 
         def finish(a):
             ot = ostage.tile([P, 512], F32, tag="ot", name="ot%d" % a)
-            if a in (5, 7):
+            if a in (5, 6):
                 nc.vector.tensor_copy(out=ot[:], in_=accs[a][:])
             else:
                 nc.scalar.copy(out=ot[:], in_=accs[a][:])
@@ -524,7 +529,7 @@ def tile_hierarchicalclustering_pa_t_kernel(tc, task_embedding, centers1, W1, b1
         def quant(lo, n):
             v_qp(NG - 1, lo, n)
             mark_p(NG - 1, lo // P, (lo + n) // P)
-            pool_some(100)
+            pool_upto((lo + n) // P + 2)
 
         d_scalar(NG - 1, 896, 128)
         d_piece(nc.vector, NG - 1, 0, 128)
@@ -546,7 +551,7 @@ def tile_hierarchicalclustering_pa_t_kernel(tc, task_embedding, centers1, W1, b1
         quant(640, 128)
         finish(4)
         quant(768, 128)
-        finish(5)
         quant(896, 128)
+        finish(5)
         finish(6)
         finish(7)

@@ -191,6 +191,14 @@ def tile_hierarchicalclustering_pa_t_kernel(tc, task_embedding, centers1, W1, b1
                 op=ALU.mult,
             )
 
+        def d_lines(g, lo, n):
+            nc.vector.tensor_tensor(
+                out=pgrps[g][:, lo : lo + n, :].rearrange("p (c i) t -> p c t i", i=4),
+                in0=ses[g][:, :, lo : lo + n].rearrange("p t (c i) -> p c t i", i=4),
+                in1=rinvs[g][:].unsqueeze(1).unsqueeze(3).to_broadcast([P, n // 4, 4, 4]),
+                op=ALU.mult,
+            )
+
         def d_scalar_t(g, lo, n, t):
             nc.scalar.activation(
                 out=pgrps[g][:, lo : lo + n, t], in_=ses[g][:, t, lo : lo + n], func=ACT.Copy,
@@ -532,22 +540,22 @@ def tile_hierarchicalclustering_pa_t_kernel(tc, task_embedding, centers1, W1, b1
             pool_upto((lo + n) // P + 2)
 
         d_scalar(NG - 1, 896, 128)
-        d_piece(nc.vector, NG - 1, 0, 128)
-        d_piece(nc.vector, NG - 1, 128, 128)
+        d_lines(NG - 1, 0, 128)
+        d_lines(NG - 1, 128, 128)
         quant(0, 128)
-        d_piece(nc.vector, NG - 1, 256, 128)
+        d_lines(NG - 1, 256, 128)
         quant(128, 128)
         finish(0)
-        d_piece(nc.vector, NG - 1, 384, 128)
+        d_lines(NG - 1, 384, 128)
         quant(256, 128)
         finish(1)
-        d_piece(nc.vector, NG - 1, 512, 128)
+        d_lines(NG - 1, 512, 128)
         quant(384, 128)
         finish(2)
-        d_piece(nc.vector, NG - 1, 640, 128)
+        d_lines(NG - 1, 640, 128)
         quant(512, 128)
         finish(3)
-        d_piece(nc.vector, NG - 1, 768, 128)
+        d_lines(NG - 1, 768, 128)
         quant(640, 128)
         finish(4)
         quant(768, 128)

from contextlib import ExitStack

import concourse.mybir as mybir
from concourse.masks import make_identity

FLOPS = 2 * 4096 * 512 * 1024 + 2 * 4096 * 512 * 512 + 2 * 4096 * 1024 * 512

F32 = mybir.dt.float32
BF16 = mybir.dt.bfloat16
U32 = mybir.dt.uint32
U8 = mybir.dt.uint8
FP8X4 = mybir.dt.float8_e4m3fn_x4
ACT = mybir.ActivationFunctionType
ALU = mybir.AluOpType
AX = mybir.AxisListType

P = 128
NG = 8
NA = 8
NS = 32
WIN = 1
SIDE = 3
G_LAST = 768
LAST_SHARE = {2: (0, 1), 3: (2, 3)}
POOL_PER_SLOT = 8


def tile_hierarchicalclustering_pa_t_kernel(tc, task_embedding, centers1, W1, b1, out):
    nc = tc.nc
    h_view = task_embedding.rearrange("(g p t) k -> g p (t k)", p=P, t=4)
    c_view = centers1.rearrange("(p a) k -> p a k", a=NA)
    w_view = W1.rearrange("(a p) k -> p a k", p=P)
    out_view = out.rearrange("(p a) d -> p a d", a=NA)

    with ExitStack() as ctx:
        ctx.enter_context(tc.manual_schedule())
        keep = ctx.enter_context(tc.tile_pool(name="keep", bufs=1))
        hpool = ctx.enter_context(tc.tile_pool(name="hpool", bufs=4))
        spool = ctx.enter_context(tc.tile_pool(name="spool", bufs=3))
        gh = ctx.enter_context(tc.tile_pool(name="gh", bufs=2))
        small = ctx.enter_context(tc.tile_pool(name="small", bufs=4))
        psum = ctx.enter_context(tc.psum_pool(name="psum", bufs=1))

        def bank(i, shape, dtype, name):
            return psum.tile(shape, dtype, tag="b%d" % i, name=name)

        ident_f = keep.tile([P, P], F32)
        ident_b = keep.tile([P, P], BF16)
        hc = keep.tile([P, NG, 512], U32, align_bytes=64)
        hs = keep.tile([P, NG, 512], U8, align_bytes=64)
        cc = keep.tile([P, 1024], U32, align_bytes=64)
        cs = keep.tile([P, 1024], U8, align_bytes=64)
        wc = keep.tile([P, 512], U32, align_bytes=64)
        ws = keep.tile([P, 512], U8, align_bytes=64)
        pc = keep.tile([P, NG, 1024], U32, align_bytes=64)
        ps = keep.tile([P, NG, 1024], U8, align_bytes=64)
        tcod = keep.tile([P, NG, 512], U32, align_bytes=64)
        tsc = keep.tile([P, NG, 512], U8, align_bytes=64)
        c4b = keep.tile([P, 1024], F32)
        b1c = keep.tile([P, 4], F32)

        hraw = {}
        hgrps = {}
        xbanks = {}
        gps = {}
        tTs = {}
        tgrps = {}
        ses = {}
        mns = {}
        sms = {}
        rinvs = {}
        pgrps = {}

        def load_h(g):
            hraw[g] = hpool.tile([P, 2048], BF16, tag="hraw", name="hraw%d" % g)
            nc.sync.dma_start(out=hraw[g][:], in_=h_view[g])

        def pe_t(g, half, b):
            hw = hraw[g][:].bitcast(F32)
            xh = bank(b, [P, 2, 2, P], F32, "xh%d_%d" % (g, half))
            for tl in range(2):
                for u in range(2):
                    lo = (2 * half + tl) * 256 + u * 128
                    nc.tensor.transpose(xh[:, tl, u, :], hw[:, lo : lo + 128], ident_f[:])
            xbanks[("t", g, half)] = xh

        def s_t(g, half):
            if half == 0:
                hgrps[g] = gh.tile([P, 2048], BF16, tag="hgrp", name="hgrp%d" % g, align_bytes=64)
            hgw = hgrps[g][:].bitcast(F32).rearrange("q (t j u) -> q t j u", t=4, u=2)
            nc.scalar.copy(
                out=hgw[:, 2 * half : 2 * half + 2, :, :],
                in_=xbanks[("t", g, half)][:].rearrange("q t u j -> q t j u"),
            )

        def v_qh(g):
            nc.vector.quantize_mx(out=hc[:, g, :].bitcast(FP8X4), scales=hs[:, g, :], in_=hgrps[g][:])

        def pe_z(g, dt, b):
            z = bank(b, [P, 512], F32, "z%d_%d" % (g, dt))
            nc.tensor.matmul_mx(
                out=z[:],
                lhsT=wc[:, dt * P : (dt + 1) * P].bitcast(FP8X4),
                lhsT_scale=ws[:, dt * P : (dt + 1) * P],
                rhs=hc[:, g, :].bitcast(FP8X4),
                rhs_scale=hs[:, g, :],
                start=True,
                stop=True,
            )
            xbanks[("z", g, dt)] = z

        def s_z(g, dt):
            if dt == 0:
                tTs[g] = grp.tile([P, 4, 2, P, 2], BF16, tag="tT", name="tT%d" % g)
            nc.scalar.activation(
                out=tTs[g][:, dt, :, :, :],
                in_=xbanks[("z", g, dt)][:].rearrange("d (u e p) -> d u p e", u=2, e=2),
                func=ACT.Tanh, bias=b1c[:, dt : dt + 1], scale=1.0,
            )

        def pe_x(g, hb, b):
            xt = bank(b, [P, 2, 256], F32, "xt%d_%d" % (g, hb))
            words = tTs[g][:].rearrange("d a u p e -> d (a u p e)").bitcast(F32)
            for dl in range(2):
                for u in range(2):
                    lo = (2 * hb + dl) * 256 + u * P
                    nc.tensor.transpose(xt[:, u, dl * P : (dl + 1) * P], words[:, lo : lo + P], ident_f[:])
            xbanks[("x", g, hb)] = xt

        def s_x(g, hb):
            if hb == 0:
                tgrps[g] = grp.tile([P, 512, 4], BF16, tag="tgrp", name="tgrp%d" % g, align_bytes=64)
            nc.scalar.copy(
                out=tgrps[g][:, hb * 256 : (hb + 1) * 256, :].bitcast(F32),
                in_=xbanks[("x", g, hb)][:].rearrange("p u d -> p d u"),
            )

        def v_qt(g):
            nc.vector.quantize_mx(
                out=tcod[:, g, :].bitcast(FP8X4), scales=tsc[:, g, :],
                in_=tgrps[g][:].rearrange("p d t -> p (d t)"),
            )

        def pe_g(s, hf):
            g, t = divmod(s, 4)
            gp = bank(hf, [P, 512], F32, "gp%d_%d" % (s, hf))
            nc.tensor.matmul_mx(
                out=gp[:],
                lhsT=hc[:, g, t * P : (t + 1) * P].bitcast(FP8X4),
                lhsT_scale=hs[:, g, t * P : (t + 1) * P],
                rhs=cc[:, hf * 512 : (hf + 1) * 512].bitcast(FP8X4),
                rhs_scale=cs[:, hf * 512 : (hf + 1) * 512],
                start=True,
                stop=True,
            )
            gps[(s, hf)] = gp

        def v_a(s, hf):
            g, t = divmod(s, 4)
            if t == 0 and hf == 0:
                ses[g] = spool.tile([P, 4, 1024], F32, tag="se", name="se%d" % g)
                mns[g] = small.tile([P, 4], F32, tag="mn", name="mn%d" % g)
            nc.vector.scalar_tensor_tensor(
                out=ses[g][:, t, hf * 512 : (hf + 1) * 512], in0=gps[(s, hf)][:], scalar=-0.5,
                in1=c4b[:, hf * 512 : (hf + 1) * 512], op0=ALU.mult, op1=ALU.add,
            )

        def v_b(s):
            g, t = divmod(s, 4)
            nc.vector.tensor_reduce(out=mns[g][:, t : t + 1], in_=ses[g][:, t, :], axis=AX.X, op=ALU.min)

        def s_c(s):
            g, t = divmod(s, 4)
            if t == 0:
                sms[g] = small.tile([P, 4], F32, tag="sm", name="sm%d" % g)
            nc.scalar.activation(
                out=ses[g][:, t, :], in_=ses[g][:, t, :], func=ACT.Exp, bias=mns[g][:, t : t + 1], scale=-1.0,
                accum_out=sms[g][:, t : t + 1],
            )

        def v_r(g):
            rinvs[g] = small.tile([P, 4], F32, tag="rinv", name="rinv%d" % g)
            nc.vector.reciprocal(rinvs[g][:], sms[g][:])
            pgrps[g] = grp.tile([P, 1024, 4], BF16, tag="pgrp", name="pgrp%d" % g, align_bytes=64)

        def d_piece(eng, g, lo, n):
            eng.tensor_tensor(
                out=pgrps[g][:, lo : lo + n, :],
                in0=ses[g][:, :, lo : lo + n].rearrange("p t i -> p i t"),
                in1=rinvs[g][:].unsqueeze(1).to_broadcast([P, n, 4]),
                op=ALU.mult,
            )

        def d_lines(g, lo, n):
            nc.vector.tensor_tensor(
                out=pgrps[g][:, lo : lo + n, :].rearrange("p (c i) t -> p c t i", i=4),
                in0=ses[g][:, :, lo : lo + n].rearrange("p t (c i) -> p c t i", i=4),
                in1=rinvs[g][:].unsqueeze(1).unsqueeze(3).to_broadcast([P, n // 4, 4, 4]),
                op=ALU.mult,
            )

        def d_scalar_t(g, lo, n, t):
            nc.scalar.activation(
                out=pgrps[g][:, lo : lo + n, t], in_=ses[g][:, t, lo : lo + n], func=ACT.Copy,
                scale=rinvs[g][:, t : t + 1],
            )

        def d_scalar(g, lo, n):
            for t in range(4):
                d_scalar_t(g, lo, n, t)

        def v_qp(g, lo, n):
            nc.vector.quantize_mx(
                out=pc[:, g, lo : lo + n].bitcast(FP8X4), scales=ps[:, g, lo : lo + n],
                in_=pgrps[g][:, lo : lo + n, :].rearrange("p i t -> p (i t)"),
            )

        accs = {}
        done = {}

        def pool_pass(a, g):
            nc.tensor.matmul_mx(
                out=accs[a][:],
                lhsT=pc[:, g, a * P : (a + 1) * P].bitcast(FP8X4),
                lhsT_scale=ps[:, g, a * P : (a + 1) * P],
                rhs=tcod[:, g, :].bitcast(FP8X4),
                rhs_scale=tsc[:, g, :],
                start=(g == 0),
                stop=(g == NG - 1),
            )
            done[a] = g + 1

        def open_acc(a, b):
            accs[a] = bank(b, [P, 512], F32, "acc%d" % a)
            done[a] = 0

        ready = {"p": [0] * NA, "t": 0}

        def pool_some(limit):
            n = 0
            for a in sorted(accs):
                while n < limit and done[a] < min(ready["p"][a], ready["t"]):
                    pool_pass(a, done[a])
                    n += 1

        def pool_upto(n):
            for a in range(min(n, NA)):
                while done[a] < min(ready["p"][a], ready["t"]):
                    pool_pass(a, done[a])

        def mark_p(g, a_lo, a_hi):
            for a in range(a_lo, a_hi):
                ready["p"][a] = g + 1

        def scores(s):
            v_a(s, 0)
            if s + 1 < NS:
                pe_g(s + 1, 0)
            if s > 0:
                v_b(s - 1)
            v_a(s, 1)
            if s + 1 < NS:
                pe_g(s + 1, 1)

        units = []

        def add_t(g):
            units.append((lambda b: pe_t(g, 0, b), lambda: s_t(g, 0), None))
            units.append((lambda b: pe_t(g, 1, b), lambda: s_t(g, 1), lambda: v_qh(g)))

        def add_z(g, d0):
            units.append((lambda b: pe_z(g, d0, b), lambda: s_z(g, d0), None))
            units.append((lambda b: pe_z(g, d0 + 1, b), lambda: s_z(g, d0 + 1), None))

        def qt_and_mark(g):
            v_qt(g)
            ready["t"] = g + 1

        def add_x(g):
            units.append((lambda b: pe_x(g, 0, b), lambda: s_x(g, 0), None))
            units.append((lambda b: pe_x(g, 1, b), lambda: s_x(g, 1), lambda: qt_and_mark(g)))

        add_t(1)
        add_z(0, 0)
        add_z(0, 2)
        for gam in range(1, NG):
            if gam + 1 < NG:
                add_t(gam + 1)
            add_x(gam - 1)
            add_z(gam, 0)
            add_z(gam, 2)
        add_x(NG - 1)

        state = {"pe": 0, "s": 0, "v": 0}
        vq = []

        def pe_pair(n=2):
            for i in range(n):
                if state["pe"] < len(units):
                    units[state["pe"]][0](2 + state["pe"] % SIDE)
                    state["pe"] += 1

        def s_pair(n=2):
            for i in range(n):
                if state["s"] < state["pe"]:
                    units[state["s"]][1]()
                    if units[state["s"]][2] is not None:
                        vq.append(units[state["s"]][2])
                    state["s"] += 1

        def v_pending(keep_back=0):
            while state["v"] < len(vq) - keep_back:
                vq[state["v"]]()
                state["v"] += 1

        make_identity(nc, ident_f[:])
        with tc.tile_pool(name="head", bufs=1) as head:
            zeros = head.tile([P, 512], BF16)
            nc.vector.memset(zeros[:], 0.0)
            idle = bank(7, [P, 512], F32, "idle")

            def pe_warm(n):
                for i in range(n):
                    nc.tensor.matmul(idle[:], lhsT=zeros[:, 0:P], rhs=zeros[:], start=True, stop=True)

            pe_warm(4)
            b1rows = head.tile([P, P], BF16)
            nc.gpsimd.memset(b1rows[:], 0.0)
            make_identity(nc, ident_b[:])
            c_sb = head.tile([P, NA, 512], BF16)

            def load_c(k):
                nc.sync.dma_start(out=c_sb[:, 2 * k : 2 * k + 2, :], in_=c_view[:, 2 * k : 2 * k + 2, :])

            load_c(0)
            load_c(1)
            load_h(0)
            load_c(2)
            load_c(3)
            w_sb = head.tile([P, 4, 512], BF16)
            nc.sync.dma_start(out=w_sb[:], in_=w_view)
            nc.sync.dma_start(out=b1rows[0:4, :], in_=b1.rearrange("(a p) -> a p", p=P))
            load_h(1)
            load_h(2)
            load_h(3)

            cw = c_sb[:].rearrange("p a k -> p (a k)").bitcast(F32)
            cgrp = head.tile([P, 4096], BF16, align_bytes=64)
            cgw = cgrp[:].bitcast(F32).rearrange("q (a j u) -> q a j u", a=NA, u=2)
            csq_s = head.tile([P, NA], F32)
            csq_v = head.tile([P, NA], F32)
            junk_s = head.tile([P, 512], F32)
            junk_v = head.tile([P, 512], F32)
            csqs = {}
            xcs = {}
            xrs = {}
            xws = {}

            def pe_c(k):
                xcs[k] = bank(k, [P, 2, 2, P], F32, "xc%d" % k)
                for al in range(2):
                    for u in range(2):
                        lo = (2 * k + al) * 256 + u * 128
                        nc.tensor.transpose(xcs[k][:, al, u, :], cw[:, lo : lo + 128], ident_f[:])

            def csq_scalar(a):
                nc.scalar.activation(
                    out=junk_s[:], in_=c_sb[:, a, :], func=ACT.Square, accum_out=csq_s[:, a : a + 1]
                )
                csqs[a] = csq_s

            def csq_vector(a):
                nc.vector.scalar_tensor_tensor(
                    out=junk_v[:], in0=c_sb[:, a, :], scalar=1.0, in1=c_sb[:, a, :],
                    op0=ALU.mult, op1=ALU.mult, accum_out=csq_v[:, a : a + 1],
                )
                csqs[a] = csq_v

            def pe_rep(hf):
                xrs[hf] = bank(6 + hf, [P, 4, P], F32, "xr%d" % hf)
                for al in range(4):
                    a = 4 * hf + al
                    nc.tensor.transpose(xrs[hf][:, al, :], csqs[a][:, a : a + 1].to_broadcast([P, P]), ident_f[:])

            def c_evac(eng_copy, k):
                eng_copy(out=cgw[:, 2 * k : 2 * k + 2, :, :], in_=xcs[k][:].rearrange("q a u j -> q a j u"))

            def c4b_scalar(hf):
                nc.scalar.activation(
                    out=c4b[:, hf * 512 : (hf + 1) * 512], in_=xrs[hf][:].rearrange("p a j -> p (a j)"),
                    func=ACT.Copy, scale=0.25,
                )

            def c4b_vector(hf):
                nc.vector.tensor_scalar_mul(
                    c4b[:, hf * 512 : (hf + 1) * 512], xrs[hf][:].rearrange("p a j -> p (a j)"), 0.25
                )

            def v_qc(hf):
                nc.vector.quantize_mx(
                    out=cc[:, hf * 512 : (hf + 1) * 512].bitcast(FP8X4), scales=cs[:, hf * 512 : (hf + 1) * 512],
                    in_=cgrp[:, hf * 2048 : (hf + 1) * 2048],
                )

            ww = w_sb[:].rearrange("p a k -> p (a k)").bitcast(F32)
            wgrp = head.tile([P, 2048], BF16, align_bytes=64)
            wgw = wgrp[:].bitcast(F32).rearrange("q (a j u) -> q a j u", a=4, u=2)

            def pe_w(pair, b):
                xws[pair] = bank(b, [P, 2, 2, P], F32, "xw%d" % pair)
                for al in range(2):
                    for u in range(2):
                        lo = (2 * pair + al) * 256 + u * 128
                        nc.tensor.transpose(xws[pair][:, al, u, :], ww[:, lo : lo + 128], ident_f[:])

            def s_w(pair):
                nc.scalar.copy(
                    out=wgw[:, 2 * pair : 2 * pair + 2, :, :], in_=xws[pair][:].rearrange("q a u j -> q a j u")
                )

            def pe_b1(b):
                xws["b1"] = bank(b, [P, P], BF16, "xb")
                nc.tensor.transpose(xws["b1"][:], b1rows[:], ident_b[:])

            def s_b1():
                nc.scalar.copy(out=b1c[:], in_=xws["b1"][:, 0:4])

            def v_qw():
                nc.vector.quantize_mx(out=wc[:].bitcast(FP8X4), scales=ws[:], in_=wgrp[:])

            pe_c(0)
            csq_scalar(0)
            csq_vector(1)
            pe_warm(1)
            pe_c(1)
            pe_warm(2)
            csq_scalar(2)
            csq_vector(3)
            pe_t(0, 0, 4)
            pe_t(0, 1, 5)
            pe_c(2)
            pe_c(3)
            pe_rep(0)
            pe_warm(2)
            c_evac(nc.scalar.copy, 0)
            c_evac(nc.vector.tensor_copy, 1)
            csq_scalar(4)
            csq_vector(5)
            v_qc(0)
            s_t(0, 0)
            s_t(0, 1)
            c_evac(nc.vector.tensor_copy, 2)
            csq_vector(7)
            v_qh(0)
            csq_scalar(6)
            c4b_vector(0)
            c_evac(nc.scalar.copy, 3)
            pe_w(0, 4)
            pe_w(1, 5)
            pe_warm(2)
            pe_g(0, 0)
            pe_rep(1)
            v_qc(1)
            v_a(0, 0)
            s_w(0)
            c4b_scalar(1)
            s_w(1)
            pe_g(0, 1)
            pe_g(1, 0)
            pe_pair()
            pe_b1(6)
            v_a(0, 1)
            pe_g(1, 1)
            s_b1()
            v_qw()


        grp = ctx.enter_context(tc.tile_pool(name="grp", bufs=2))
        ostage = ctx.enter_context(tc.tile_pool(name="ostage", bufs=8))

        def window(g):
            v_pending(1)
            if g >= 2:
                v_qp(g - 2, 0, 1024)
                mark_p(g - 2, 0, NA)
            v_r(g - 1)
            v_pending()

        for a in range(6 - SIDE):
            open_acc(a, 2 + SIDE + a)
        for s in range(NS):
            g, t = divmod(s, 4)
            if s > 0:
                scores(s)
            if g == 0:
                v_pending()
            elif t == WIN:
                window(g)
                d_piece(nc.gpsimd, g - 1, 0, G_LAST if g == NG - 1 else 1024)
            s_pair(3)
            if g == NG - 1 and t >= 2:
                for i in LAST_SHARE[t]:
                    d_scalar_t(g - 1, G_LAST, 1024 - G_LAST, i)
            if s > 0:
                s_c(s - 1)
            pe_pair(3 if t == 0 and 1 <= g <= 4 else 2)
            if state["s"] == len(units) and 5 not in accs:
                for a in range(6 - SIDE, 6):
                    open_acc(a, a + SIDE - 4)
            if s == 0:
                load_h(4)
                load_h(5)
            if s == 3:
                load_h(6)
            if s == 7:
                load_h(7)
            pool_some(POOL_PER_SLOT)

        v_b(NS - 1)
        s_c(NS - 1)
        open_acc(6, 0)
        open_acc(7, 1)
        pool_some(100)
        v_qp(NG - 2, 0, 1024)
        mark_p(NG - 2, 0, NA)
        pool_upto(3)
        v_r(NG - 1)

        def finish(a):
            ot = ostage.tile([P, 512], F32, tag="ot", name="ot%d" % a)
            if a in (5, 6):
                nc.vector.tensor_copy(out=ot[:], in_=accs[a][:])
            else:
                nc.scalar.copy(out=ot[:], in_=accs[a][:])
            nc.sync.dma_start(out=out_view[:, a, :], in_=ot[:])

        def quant(lo, n):
            v_qp(NG - 1, lo, n)
            mark_p(NG - 1, lo // P, (lo + n) // P)
            pool_upto((lo + n) // P + 2)

        d_scalar(NG - 1, 896, 128)
        d_lines(NG - 1, 0, 128)
        d_lines(NG - 1, 128, 128)
        quant(0, 128)
        d_lines(NG - 1, 256, 128)
        quant(128, 128)
        finish(0)
        d_lines(NG - 1, 384, 128)
        quant(256, 128)
        finish(1)
        d_lines(NG - 1, 512, 128)
        quant(384, 128)
        finish(2)
        d_lines(NG - 1, 640, 128)
        quant(512, 128)
        finish(3)
        d_lines(NG - 1, 768, 128)
        quant(640, 128)
        finish(4)
        quant(768, 128)
        quant(896, 128)
        finish(5)
        finish(6)
        finish(7)
